import numpy as np
import ml_dtypes


def mxq(x, axis, fmt="e4m3"):
    dtype, down = {"e4m3": (ml_dtypes.float8_e4m3fn, 7), "e5m2": (ml_dtypes.float8_e5m2, 14)}[fmt]
    v = np.moveaxis(np.asarray(x, np.float32).astype(ml_dtypes.bfloat16).astype(np.float64), axis, -1)
    blocks = v.reshape(v.shape[:-1] + (-1, 32))
    amax = np.abs(blocks).max(-1, keepdims=True)
    byte = np.maximum(np.where(amax > 0, np.frexp(amax)[1] - 1 + 127, 0) - down, 1)
    scale = np.exp2(byte - 127.0)
    codes = (blocks / scale).astype(np.float32).astype(dtype).astype(np.float64)
    return np.moveaxis((codes * scale).reshape(v.shape), -1, axis)


WIDE = False


def mx_kscale(k):
    if not WIDE:
        return np.ones(k)
    levels = np.array([10, -10, 5, -5, 0])
    if k % 512:
        return np.exp2(np.random.permutation(np.resize(levels, k // 32))).repeat(32)
    a = np.empty((k // 512, 16))
    for p in range(k // 512):
        a[p, :8] = np.random.permutation(np.resize(levels, 8))
        for g in range(8):
            far = levels[np.abs(levels - a[p, g]) >= 10]
            a[p, g + 8] = far[np.random.randint(len(far))]
    return np.exp2(a.ravel()).repeat(32)


BF16 = ml_dtypes.bfloat16


def bf(x):
    return np.asarray(x, np.float32).astype(BF16)


def f64(x):
    return np.asarray(x).astype(np.float64)


B, T, M, H, D, QB = 4, 512, 1024, 8, 128, 512
ROTARY_BASE = 10000.0
HALF = D // 2
HD = H * D


def rope(u):
    positions = f64(np.arange(T))
    dims = f64(np.arange(HALF))
    ang_freqs = np.power(ROTARY_BASE, -dims / HALF)
    radians = positions[:, None] * ang_freqs[None, :]
    cos = np.cos(radians)[None, :, None, :]
    sin = np.sin(radians)[None, :, None, :]
    even, odd = u[..., :HALF], u[..., HALF:]
    return np.concatenate([even * cos - odd * sin, even * sin + odd * cos], axis=-1)


def draw0():
    s = mx_kscale(M)
    return {"x": bf(np.random.standard_normal((B, T, M)) * s),
            "w_aq": bf(np.random.standard_normal((M, H, D)) * 2.5 / np.sqrt(M) / s[:, None, None]),
            "w_ak": bf(np.random.standard_normal((M, H, D)) * 2.5 / np.sqrt(M) / s[:, None, None])}


def core(x, w_aq, w_ak):
    xq = mxq(f64(x), 2, "e4m3")
    q = (xq @ mxq(f64(w_aq).reshape(M, HD), 0, "e4m3")).reshape(B, T, H, D)
    k = (xq @ mxq(f64(w_ak).reshape(M, HD), 0, "e4m3")).reshape(B, T, H, D)
    return rope(q), rope(k)


def e4m3fn_bytes(y):
    return np.clip(np.asarray(y, np.float64), -448.0, 448.0).astype(np.float32).astype(ml_dtypes.float8_e4m3fn).view(np.uint8)


def e4m3fn_values(b):
    return np.asarray(b, np.uint8).view(ml_dtypes.float8_e4m3fn).astype(np.float64)


def setup_inputs():
    d = draw0()
    x0 = np.asarray(d['x']).astype(np.float64)
    s = (np.max(np.abs(x0), axis=(0, 1), keepdims=True) / 448.0).astype(np.float32)
    out = {}
    for k, v in d.items():
        if k == 'x':
            out['x_bytes'] = e4m3fn_bytes(x0 / s.astype(np.float64))
            out['x_scale'] = s
        else:
            out[k] = v
    return out


def reference(x_bytes, x_scale, w_aq, w_ak):
    return core(e4m3fn_values(x_bytes) * x_scale.astype(np.float64), w_aq, w_ak)

@@ -1,0 +1,303 @@
+from contextlib import ExitStack
+
+import concourse.mybir as mybir
+from concourse.masks import make_identity
+
+B, T, M, H, D = 4, 512, 1024, 8, 128
+HD = H * D
+FLOPS = 2 * (B * T) * M * (2 * HD)
+
+F32 = mybir.dt.float32
+BF16 = mybir.dt.bfloat16
+I32 = mybir.dt.int32
+U32 = mybir.dt.uint32
+U8 = mybir.dt.uint8
+FP8 = mybir.dt.float8_e4m3fn
+FP8X4 = mybir.dt.float8_e4m3fn_x4
+ALU = mybir.AluOpType
+ACT = mybir.ActivationFunctionType
+ENG = mybir.EngineType
+
+P = 128
+NT = 4
+G = 2
+CH = 512
+HALF = D // 2
+RATIO = 10000.0 ** (-1.0 / HALF)
+PI = 3.141592653589793
+TWO_PI = 2.0 * PI
+
+SETS = [(0, 0, 1), (0, 1, 1), (0, 2, 2)] + [(b, i0, 2) for b in range(1, B) for i0 in (0, 2)]
+X_CAST_ON_VECTOR = (1, 2)
+X_INTER_ON_GPSIMD = (0, 1, 2)
+W_INTER_ON_VECTOR = ((0, 0),)
+
+
+def tile_multiheadselfattention_pa_kernel(tc, x_bytes, x_scale, w_aq, w_ak, out_0, out_1):
+    nc = tc.nc
+    with ExitStack() as ctx:
+        const = ctx.enter_context(tc.tile_pool(name="const", bufs=1))
+        xb_pool = ctx.enter_context(tc.tile_pool(name="xb", bufs=3))
+        wr_pool = ctx.enter_context(tc.tile_pool(name="wr", bufs=4))
+        xw_pool = ctx.enter_context(tc.tile_pool(name="xw", bufs=3))
+        xp_pool = ctx.enter_context(tc.tile_pool(name="xp", bufs=3))
+        xg_pool = ctx.enter_context(tc.tile_pool(name="xg", bufs=3))
+        wg_pool = ctx.enter_context(tc.tile_pool(name="wg", bufs=2))
+        xy_pool = ctx.enter_context(tc.tile_pool(name="xy", bufs=6))
+        o_pool = ctx.enter_context(tc.tile_pool(name="o", bufs=4))
+        psx = ctx.enter_context(tc.psum_pool(name="psx", bufs=3))
+        psu = ctx.enter_context(tc.psum_pool(name="psu", bufs=5))
+
+        xv = x_bytes.rearrange("b (p i) k -> b p (i k)", i=NT)
+        wv = [w.rearrange("(g p j) h d -> g p j (h d)", g=G, p=P, j=4) for w in (w_aq, w_ak)]
+        ov = [o.rearrange("b (p i) h d -> b i p (h d)", i=NT) for o in (out_0, out_1)]
+
+        xb_of = {}
+        wr = {}
+
+        def load_x(key, b, lo, hi):
+            xb_of[key] = xb_pool.tile([P, hi - lo], U8, name="xbytes", tag="xbytes")
+            nc.sync.dma_start(out=xb_of[key][:], in_=xv[b][:, lo:hi])
+
+        def load_w(m, c):
+            for g in range(G):
+                wr[(m, g, c)] = wr_pool.tile([P, 4, CH], BF16, name="wr", tag="wr")
+                nc.sync.dma_start(out=wr[(m, g, c)][:], in_=wv[m][g][:, :, c * CH:(c + 1) * CH])
+
+        def bytes_of(b, i0, n):
+            if b > 0:
+                return xb_of[b][:, i0 * M:(i0 + n) * M]
+            if i0 == 0:
+                return xb_of["a"][:]
+            return xb_of["b"][:, (i0 - 1) * M:(i0 - 1 + n) * M]
+
+        xs = const.tile([P, G, 4], F32, name="xs")
+        load_x("a", 0, 0, M)
+        nc.sync.dma_start(out=xs[:], in_=x_scale[0, 0, :].rearrange("(g p t) -> p g t", g=G, p=P, t=4))
+        load_x("b", 0, M, NT * M)
+        load_w(0, 0)
+        load_w(0, 1)
+
+        xw_of = {}
+        xbank_of = {}
+        xp_of = {}
+        xg_of = {}
+        xc_of = {}
+
+        def x_cast(s):
+            b, i0, n = SETS[s]
+            xw_of[s] = xw_pool.tile([P, n * M], BF16, name="xw", tag="xw")
+            if s in X_CAST_ON_VECTOR:
+                nc.vector.tensor_copy(out=xw_of[s][:], in_=bytes_of(b, i0, n).bitcast(FP8))
+            else:
+                nc.scalar.copy(out=xw_of[s][:], in_=bytes_of(b, i0, n).bitcast(FP8))
+
+        def x_transpose(s):
+            b, i0, n = SETS[s]
+            R = n * P
+            words = xw_of[s][:].bitcast(F32)
+            per = 4 // n
+            banks = []
+            for q in range(4):
+                g, u = q // 2, q % 2
+                if q % per == 0:
+                    bank = psx.tile([P, CH], F32, name="xbank", tag="xbank")
+                    banks.append(bank)
+                off = (q % per) * R
+                for ii in range(n):
+                    lo = ii * (M // 2) + 256 * g + u
+                    nc.tensor.transpose(banks[-1][:, off + ii * P:off + (ii + 1) * P],
+                                        words[:, lo:ii * (M // 2) + 256 * (g + 1):2], ident[:])
+            xbank_of[s] = banks
+
+        def x_evac(s):
+            b, i0, n = SETS[s]
+            R = n * P
+            per = 4 // n
+            xp = xp_pool.tile([P, G, 4, R], BF16, name="xp", tag="xp")
+            for q in range(4):
+                g, u = q // 2, q % 2
+                off = (q % per) * R
+                pairs = xbank_of[s][q // per][:, off:off + R].bitcast(BF16).rearrange("p (r e) -> p r e", e=2)
+                for e in range(2):
+                    t = 2 * u + e
+                    nc.scalar.activation(out=xp[:, g, t, :], in_=pairs[:, :, e], func=ACT.Copy,
+                                         scale=xs[:, g, t:t + 1])
+            xp_of[s] = xp
+
+        def x_inter(s):
+            b, i0, n = SETS[s]
+            R = n * P
+            xp = xp_of[s]
+            xg = xg_pool.tile([P, G, R, 4], BF16, name="xg", tag="xg", align_bytes=64)
+            for g in range(G):
+                src = xp[:, g].rearrange("p t r -> p r t")
+                if s in X_INTER_ON_GPSIMD:
+                    nc.gpsimd.tensor_scalar(out=xg[:, g], in0=src, scalar1=1.0, scalar2=0.0,
+                                            op0=ALU.mult, op1=ALU.add)
+                else:
+                    nc.scalar.copy(out=xg[:, g], in_=src)
+            xg_of[s] = xg
+
+        def x_quant(s):
+            b, i0, n = SETS[s]
+            R = n * P
+            xc = const.tile([P, G, R], U32, name="xc%d" % s, align_bytes=64)
+            xsc = const.tile([P, G, R], U8, name="xsc%d" % s, align_bytes=64)
+            nc.vector.quantize_mx(out=xc[:].rearrange("p g r -> p (g r)").bitcast(FP8X4),
+                                  scales=xsc[:].rearrange("p g r -> p (g r)"),
+                                  in_=xg_of[s][:].rearrange("p g r t -> p (g r t)"))
+            for ii in range(n):
+                xc_of[(b, i0 + ii)] = (xc, xsc, ii * P)
+
+        wg_of = {}
+        wc_of = {}
+
+        def w_inter(m, c):
+            wg = wg_pool.tile([P, G, CH, 4], BF16, name="wg", tag="wg", align_bytes=64)
+            for g in range(G):
+                src = wr[(m, g, c)][:].rearrange("p j n -> p n j")
+                if (m, c) in W_INTER_ON_VECTOR:
+                    nc.vector.tensor_copy(out=wg[:, g], in_=src)
+                else:
+                    nc.scalar.copy(out=wg[:, g], in_=src)
+            wg_of[(m, c)] = wg
+
+        def w_quant(m, c):
+            wc = const.tile([P, G, CH], U32, name="wc%d%d" % (m, c), align_bytes=64)
+            wsc = const.tile([P, G, CH], U8, name="wsc%d%d" % (m, c), align_bytes=64)
+            nc.vector.quantize_mx(out=wc[:].rearrange("p g n -> p (g n)").bitcast(FP8X4),
+                                  scales=wsc[:].rearrange("p g n -> p (g n)"),
+                                  in_=wg_of[(m, c)][:].rearrange("p g n j -> p (g n j)"))
+            wc_of[(m, c)] = (wc, wsc)
+
+        def span(b, i, m, cs, add_on_vector=False):
+            xc, xsc, off = xc_of[(b, i)]
+            nh = 4 * len(cs)
+            xy = xy_pool.tile([P, 2, nh, 2, HALF], F32, name="xy", tag="xy")
+            for k, c in enumerate(cs):
+                wc, wsc = wc_of[(m, c)]
+                acc = psu.tile([P, CH], F32, name="acc", tag="acc")
+                for g in range(G):
+                    nc.tensor.matmul_mx(out=acc[:],
+                                        lhsT=xc[:, g, off:off + P].bitcast(FP8X4), lhsT_scale=xsc[:, g, off:off + P],
+                                        rhs=wc[:, g, :].bitcast(FP8X4), rhs_scale=wsc[:, g, :],
+                                        start=(g == 0), stop=(g == G - 1))
+                for v in range(2):
+                    nc.vector.tensor_tensor(out=xy[:, v, 4 * k:4 * k + 4].rearrange("p h s j -> p h (s j)"),
+                                            in0=acc[:].rearrange("p (h d) -> p h d", d=D),
+                                            in1=tab[:, i, v, :].unsqueeze(1).to_broadcast([P, 4, D]), op=ALU.mult)
+            o = o_pool.tile([P, nh * D], F32, name="o", tag="o")
+            eng = nc.vector if add_on_vector else nc.gpsimd
+            eng.tensor_tensor(out=o[:].rearrange("p (h v j) -> p h v j", v=2, j=HALF),
+                              in0=xy[:, :, :, 0, :].rearrange("p v h j -> p h v j"),
+                              in1=xy[:, :, :, 1, :].rearrange("p v h j -> p h v j"),
+                              op=ALU.add)
+            nc.sync.dma_start(out=ov[m][b, i][:, cs[0] * CH:(cs[-1] + 1) * CH], in_=o[:])
+
+        ident = const.tile([P, P], F32, name="ident")
+        warm = const.tile([P, 1], F32, name="warm")
+        pos = const.tile([P, NT, 1], I32, name="pos")
+        ang = const.tile([P, NT, HALF], F32, name="ang")
+        turns = const.tile([P, NT, HALF], I32, name="turns")
+        red = const.tile([P, NT, HALF], F32, name="red")
+        sh = const.tile([P, NT, HALF], F32, name="sh")
+        mag = const.tile([P, NT, HALF], F32, name="mag")
+        hc = const.tile([P, NT, HALF], F32, name="hc")
+        chh = const.tile([P, NT, HALF], F32, name="chh")
+        sq = const.tile([P, NT, HALF], F32, name="sq")
+        tab = const.tile([P, NT, 2, D], F32, name="tab")
+
+        with tc.manual_schedule(engines={ENG.PE, ENG.DVE, ENG.Activation, ENG.Pool}):
+            nc.gpsimd.iota(pos[:], pattern=[[1, NT]], base=0, channel_multiplier=NT)
+            make_identity(nc, ident[:])
+            nc.vector.memset(warm[:], 0.0)
+            nc.scalar.activation(out=warm[:], in_=warm[:], func=ACT.Sin)
+            nc.vector.tensor_copy(out=ang[:, :, 0:1], in_=pos[:])
+            for k in range(6):
+                w = 2 ** k
+                nc.vector.tensor_scalar(out=ang[:, :, w:2 * w], in0=ang[:, :, 0:w], scalar1=RATIO ** w,
+                                        scalar2=None, op0=ALU.mult)
+            nc.vector.tensor_scalar(out=turns[:], in0=ang[:], scalar1=1.0 / TWO_PI, scalar2=0.25,
+                                    op0=ALU.mult, op1=ALU.add)
+            nc.vector.scalar_tensor_tensor(out=red[:], in0=turns[:], scalar=-TWO_PI, in1=ang[:],
+                                           op0=ALU.mult, op1=ALU.add)
+            nc.vector.scalar_tensor_tensor(out=mag[:], in0=red[:], scalar=-1.0, in1=red[:],
+                                           op0=ALU.mult, op1=ALU.max)
+            nc.vector.tensor_scalar(out=hc[:], in0=mag[:], scalar1=-0.5, scalar2=0.5 * PI,
+                                    op0=ALU.mult, op1=ALU.add)
+            x_cast(0)
+            nc.scalar.activation(out=sh[:], in_=red[:], func=ACT.Sin, scale=0.5)
+            nc.scalar.activation(out=chh[:], in_=hc[:], func=ACT.Sin)
+            x_transpose(0)
+            x_cast(1)
+            x_cast(2)
+            nc.vector.scalar_tensor_tensor(out=sq[:], in0=sh[:], scalar=-2.0, in1=sh[:], op0=ALU.mult, op1=ALU.mult)
+            nc.vector.tensor_scalar(out=tab[:, :, 0, 0:HALF], in0=sq[:], scalar1=1.0, scalar2=None, op0=ALU.add)
+            nc.vector.tensor_scalar(out=tab[:, :, 1, HALF:D], in0=sq[:], scalar1=1.0, scalar2=None, op0=ALU.add)
+            nc.vector.scalar_tensor_tensor(out=tab[:, :, 1, 0:HALF], in0=sh[:], scalar=2.0, in1=chh[:],
+                                           op0=ALU.mult, op1=ALU.mult)
+            nc.vector.scalar_tensor_tensor(out=tab[:, :, 0, HALF:D], in0=sh[:], scalar=-2.0, in1=chh[:],
+                                           op0=ALU.mult, op1=ALU.mult)
+            x_transpose(1)
+            x_evac(0)
+            x_transpose(2)
+            x_evac(1)
+            x_evac(2)
+            x_inter(0)
+            x_inter(1)
+            x_inter(2)
+            w_inter(0, 0)
+            x_quant(0)
+            w_quant(0, 0)
+            span(0, 0, 0, [0])
+            x_quant(1)
+            span(0, 1, 0, [0])
+            x_quant(2)
+            span(0, 2, 0, [0])
+            span(0, 3, 0, [0])
+
+        load_w(1, 0)
+        load_x(1, 1, 0, NT * M)
+        load_w(1, 1)
+        w_inter(0, 1)
+        w_quant(0, 1)
+        w_inter(1, 0)
+        for i in range(NT):
+            span(0, i, 0, [1])
+        w_quant(1, 0)
+        w_inter(1, 1)
+        x_cast(3)
+        x_transpose(3)
+        x_evac(3)
+        load_x(2, 2, 0, NT * M)
+        for i in range(NT):
+            span(0, i, 1, [0])
+        w_quant(1, 1)
+        x_inter(3)
+        x_quant(3)
+        x_cast(4)
+        x_transpose(4)
+        x_evac(4)
+        for i in range(NT):
+            span(0, i, 1, [1])
+        load_x(3, 3, 0, NT * M)
+        last = len(SETS) - 1
+        for s in range(3, len(SETS)):
+            b, i0, n = SETS[s]
+            if s + 1 < len(SETS):
+                x_inter(s + 1)
+                x_quant(s + 1)
+            if s + 2 < len(SETS):
+                x_cast(s + 2)
+                x_transpose(s + 2)
+                x_evac(s + 2)
+            for ii in range(n):
+                i = i0 + ii
+                if s == last and ii == n - 1:
+                    span(b, i, 0, [0, 1])
+                    span(b, i, 1, [0])
+                    span(b, i, 1, [1], add_on_vector=True)
+                else:
+                    span(b, i, 0, [0, 1])
+                    span(b, i, 1, [0, 1])

@@ -174,7 +174,7 @@ def tile_multiheadselfattention_pa_kernel(tc, x_bytes, x_scale, w_aq, w_ak, out_
         def span(b, i, m, cs, add_on_vector=False):
             xc, xsc, off = xc_of[(b, i)]
             nh = 4 * len(cs)
-            xy = xy_pool.tile([P, 2, nh, 2, HALF], F32, name="xy", tag="xy")
+            xy = xy_pool.tile([P, nh, 2, D], F32, name="xy", tag="xy")
             for k, c in enumerate(cs):
                 wc, wsc = wc_of[(m, c)]
                 acc = psu.tile([P, CH], F32, name="acc", tag="acc")
@@ -183,16 +183,14 @@ def tile_multiheadselfattention_pa_kernel(tc, x_bytes, x_scale, w_aq, w_ak, out_
                                         lhsT=xc[:, g, off:off + P].bitcast(FP8X4), lhsT_scale=xsc[:, g, off:off + P],
                                         rhs=wc[:, g, :].bitcast(FP8X4), rhs_scale=wsc[:, g, :],
                                         start=(g == 0), stop=(g == G - 1))
-                for v in range(2):
-                    nc.vector.tensor_tensor(out=xy[:, v, 4 * k:4 * k + 4].rearrange("p h s j -> p h (s j)"),
-                                            in0=acc[:].rearrange("p (h d) -> p h d", d=D),
-                                            in1=tab[:, i, v, :].unsqueeze(1).to_broadcast([P, 4, D]), op=ALU.mult)
+                nc.vector.tensor_tensor(out=xy[:, 4 * k:4 * k + 4].rearrange("p h q d -> p (h q d)"),
+                                        in0=acc[:].rearrange("p (a j) -> p a j", j=HALF).unsqueeze(2).to_broadcast([P, 8, 2, HALF]),
+                                        in1=tab[:, i].rearrange("p q d -> p (q d)").unsqueeze(1).to_broadcast([P, 4, 2 * D]),
+                                        op=ALU.mult)
             o = o_pool.tile([P, nh * D], F32, name="o", tag="o")
             eng = nc.vector if add_on_vector else nc.gpsimd
-            eng.tensor_tensor(out=o[:].rearrange("p (h v j) -> p h v j", v=2, j=HALF),
-                              in0=xy[:, :, :, 0, :].rearrange("p v h j -> p h v j"),
-                              in1=xy[:, :, :, 1, :].rearrange("p v h j -> p h v j"),
-                              op=ALU.add)
+            eng.tensor_tensor(out=o[:].rearrange("p (h d) -> p h d", d=D),
+                              in0=xy[:, :, 0, :], in1=xy[:, :, 1, :], op=ALU.add)
             nc.sync.dma_start(out=ov[m][b, i][:, cs[0] * CH:(cs[-1] + 1) * CH], in_=o[:])
 
         ident = const.tile([P, P], F32, name="ident")
@@ -235,9 +233,9 @@ def tile_multiheadselfattention_pa_kernel(tc, x_bytes, x_scale, w_aq, w_ak, out_
             nc.vector.scalar_tensor_tensor(out=sq[:], in0=sh[:], scalar=-2.0, in1=sh[:], op0=ALU.mult, op1=ALU.mult)
             nc.vector.tensor_scalar(out=tab[:, :, 0, 0:HALF], in0=sq[:], scalar1=1.0, scalar2=None, op0=ALU.add)
             nc.vector.tensor_scalar(out=tab[:, :, 1, HALF:D], in0=sq[:], scalar1=1.0, scalar2=None, op0=ALU.add)
-            nc.vector.scalar_tensor_tensor(out=tab[:, :, 1, 0:HALF], in0=sh[:], scalar=2.0, in1=chh[:],
+            nc.vector.scalar_tensor_tensor(out=tab[:, :, 0, HALF:D], in0=sh[:], scalar=2.0, in1=chh[:],
                                            op0=ALU.mult, op1=ALU.mult)
-            nc.vector.scalar_tensor_tensor(out=tab[:, :, 0, HALF:D], in0=sh[:], scalar=-2.0, in1=chh[:],
+            nc.vector.scalar_tensor_tensor(out=tab[:, :, 1, 0:HALF], in0=sh[:], scalar=-2.0, in1=chh[:],
                                            op0=ALU.mult, op1=ALU.mult)
             x_transpose(1)
             x_evac(0)

@@ -43,8 +43,8 @@ def tile_multiheadselfattention_pa_kernel(tc, x_bytes, x_scale, w_aq, w_ak, out_
         xp_pool = ctx.enter_context(tc.tile_pool(name="xp", bufs=3))
         xg_pool = ctx.enter_context(tc.tile_pool(name="xg", bufs=3))
         wg_pool = ctx.enter_context(tc.tile_pool(name="wg", bufs=2))
-        xy_pool = ctx.enter_context(tc.tile_pool(name="xy", bufs=6))
-        o_pool = ctx.enter_context(tc.tile_pool(name="o", bufs=4))
+        xy_pool = ctx.enter_context(tc.tile_pool(name="xy", bufs=4))
+        o_pool = ctx.enter_context(tc.tile_pool(name="o", bufs=5))
         psx = ctx.enter_context(tc.psum_pool(name="psx", bufs=3))
         psu = ctx.enter_context(tc.psum_pool(name="psu", bufs=5))
 
@@ -171,11 +171,11 @@ def tile_multiheadselfattention_pa_kernel(tc, x_bytes, x_scale, w_aq, w_ak, out_
                                   in_=wg_of[(m, c)][:].rearrange("p g n j -> p (g n j)"))
             wc_of[(m, c)] = (wc, wsc)
 
-        def span(b, i, m, cs, add_on_vector=False):
-            xc, xsc, off = xc_of[(b, i)]
-            nh = 4 * len(cs)
+        def span(b, banks, add_on_vector=False):
+            nh = 4 * len(banks)
             xy = xy_pool.tile([P, nh, 2, D], F32, name="xy", tag="xy")
-            for k, c in enumerate(cs):
+            for k, (i, m, c) in enumerate(banks):
+                xc, xsc, off = xc_of[(b, i)]
                 wc, wsc = wc_of[(m, c)]
                 acc = psu.tile([P, CH], F32, name="acc", tag="acc")
                 for g in range(G):
@@ -191,7 +191,14 @@ def tile_multiheadselfattention_pa_kernel(tc, x_bytes, x_scale, w_aq, w_ak, out_
             eng = nc.vector if add_on_vector else nc.gpsimd
             eng.tensor_tensor(out=o[:].rearrange("p (h d) -> p h d", d=D),
                               in0=xy[:, :, 0, :], in1=xy[:, :, 1, :], op=ALU.add)
-            nc.sync.dma_start(out=ov[m][b, i][:, cs[0] * CH:(cs[-1] + 1) * CH], in_=o[:])
+            k = 0
+            while k < len(banks):
+                i, m, c = banks[k]
+                n = 1
+                while k + n < len(banks) and banks[k + n] == (i, m, c + n):
+                    n += 1
+                nc.sync.dma_start(out=ov[m][b, i][:, c * CH:(c + n) * CH], in_=o[:, k * CH:(k + n) * CH])
+                k += n
 
         ident = const.tile([P, P], F32, name="ident")
         warm = const.tile([P, 1], F32, name="warm")
@@ -248,12 +255,11 @@ def tile_multiheadselfattention_pa_kernel(tc, x_bytes, x_scale, w_aq, w_ak, out_
             w_inter(0, 0)
             x_quant(0)
             w_quant(0, 0)
-            span(0, 0, 0, [0])
+            span(0, [(0, 0, 0)])
             x_quant(1)
-            span(0, 1, 0, [0])
+            span(0, [(1, 0, 0)])
             x_quant(2)
-            span(0, 2, 0, [0])
-            span(0, 3, 0, [0])
+            span(0, [(2, 0, 0), (3, 0, 0)])
 
         load_w(1, 0)
         load_x(1, 1, 0, NT * M)
@@ -261,24 +267,24 @@ def tile_multiheadselfattention_pa_kernel(tc, x_bytes, x_scale, w_aq, w_ak, out_
         w_inter(0, 1)
         w_quant(0, 1)
         w_inter(1, 0)
-        for i in range(NT):
-            span(0, i, 0, [1])
+        for i in (0, 2):
+            span(0, [(i, 0, 1), (i + 1, 0, 1)])
         w_quant(1, 0)
         w_inter(1, 1)
         x_cast(3)
         x_transpose(3)
         x_evac(3)
         load_x(2, 2, 0, NT * M)
-        for i in range(NT):
-            span(0, i, 1, [0])
+        for i in (0, 2):
+            span(0, [(i, 1, 0), (i + 1, 1, 0)])
         w_quant(1, 1)
         x_inter(3)
         x_quant(3)
         x_cast(4)
         x_transpose(4)
         x_evac(4)
-        for i in range(NT):
-            span(0, i, 1, [1])
+        for i in (0, 2):
+            span(0, [(i, 1, 1), (i + 1, 1, 1)])
         load_x(3, 3, 0, NT * M)
         last = len(SETS) - 1
         for s in range(3, len(SETS)):
@@ -293,9 +299,11 @@ def tile_multiheadselfattention_pa_kernel(tc, x_bytes, x_scale, w_aq, w_ak, out_
             for ii in range(n):
                 i = i0 + ii
                 if s == last and ii == n - 1:
-                    span(b, i, 0, [0, 1])
-                    span(b, i, 1, [0])
-                    span(b, i, 1, [1], add_on_vector=True)
+                    span(b, [(i, 0, 0), (i, 0, 1)])
+                    span(b, [(i, 1, 0)])
+                    span(b, [(i, 1, 1)], add_on_vector=True)
+                elif s == last:
+                    span(b, [(i, 0, 0), (i, 0, 1)])
+                    span(b, [(i, 1, 0), (i, 1, 1)])
                 else:
-                    span(b, i, 0, [0, 1])
-                    span(b, i, 1, [0, 1])
+                    span(b, [(i, 0, 0), (i, 0, 1), (i, 1, 0), (i, 1, 1)])

@@ -27,10 +27,10 @@ RATIO = 10000.0 ** (-1.0 / HALF)
 PI = 3.141592653589793
 TWO_PI = 2.0 * PI
 
-SETS = [(0, 0, 1), (0, 1, 1), (0, 2, 2)] + [(b, i0, 2) for b in range(1, B) for i0 in (0, 2)]
-X_CAST_ON_VECTOR = (1, 2)
-X_INTER_ON_GPSIMD = (0, 1, 2)
-W_INTER_ON_VECTOR = ((0, 0),)
+SETS = [(0, i, 1) for i in range(NT)] + [(b, i0, 2) for b in range(1, B) for i0 in (0, 2)]
+X_CAST_ON_VECTOR = (1, 2, 3)
+X_INTER_ON_GPSIMD = (0, 1, 2, 3)
+W_INTER_ON_VECTOR = ((0, 0, 0), (0, 0, 1), (0, 1, 1))
 
 
 def tile_multiheadselfattention_pa_kernel(tc, x_bytes, x_scale, w_aq, w_ak, out_0, out_1):
@@ -157,7 +157,7 @@ def tile_multiheadselfattention_pa_kernel(tc, x_bytes, x_scale, w_aq, w_ak, out_
             wg = wg_pool.tile([P, G, CH, 4], BF16, name="wg", tag="wg", align_bytes=64)
             for g in range(G):
                 src = wr[(m, g, c)][:].rearrange("p j n -> p n j")
-                if (m, c) in W_INTER_ON_VECTOR:
+                if (m, c, g) in W_INTER_ON_VECTOR:
                     nc.vector.tensor_copy(out=wg[:, g], in_=src)
                 else:
                     nc.scalar.copy(out=wg[:, g], in_=src)
@@ -237,6 +237,7 @@ def tile_multiheadselfattention_pa_kernel(tc, x_bytes, x_scale, w_aq, w_ak, out_
             x_transpose(0)
             x_cast(1)
             x_cast(2)
+            x_cast(3)
             nc.vector.scalar_tensor_tensor(out=sq[:], in0=sh[:], scalar=-2.0, in1=sh[:], op0=ALU.mult, op1=ALU.mult)
             nc.vector.tensor_scalar(out=tab[:, :, 0, 0:HALF], in0=sq[:], scalar1=1.0, scalar2=None, op0=ALU.add)
             nc.vector.tensor_scalar(out=tab[:, :, 1, HALF:D], in0=sq[:], scalar1=1.0, scalar2=None, op0=ALU.add)
@@ -248,46 +249,50 @@ def tile_multiheadselfattention_pa_kernel(tc, x_bytes, x_scale, w_aq, w_ak, out_
             x_evac(0)
             x_transpose(2)
             x_evac(1)
+            x_transpose(3)
             x_evac(2)
-            x_inter(0)
-            x_inter(1)
-            x_inter(2)
+            x_evac(3)
+            for s in range(NT):
+                x_inter(s)
             w_inter(0, 0)
             x_quant(0)
             w_quant(0, 0)
-            span(0, [(0, 0, 0)])
             x_quant(1)
-            span(0, [(1, 0, 0)])
+            w_inter(0, 1)
+            span(0, [(0, 0, 0)])
             x_quant(2)
+            span(0, [(1, 0, 0)])
+            x_quant(3)
+            w_quant(0, 1)
             span(0, [(2, 0, 0), (3, 0, 0)])
 
         load_w(1, 0)
         load_x(1, 1, 0, NT * M)
         load_w(1, 1)
-        w_inter(0, 1)
-        w_quant(0, 1)
-        w_inter(1, 0)
-        for i in (0, 2):
-            span(0, [(i, 0, 1), (i + 1, 0, 1)])
-        w_quant(1, 0)
-        w_inter(1, 1)
-        x_cast(3)
-        x_transpose(3)
-        x_evac(3)
-        load_x(2, 2, 0, NT * M)
-        for i in (0, 2):
-            span(0, [(i, 1, 0), (i + 1, 1, 0)])
-        w_quant(1, 1)
-        x_inter(3)
-        x_quant(3)
-        x_cast(4)
-        x_transpose(4)
-        x_evac(4)
-        for i in (0, 2):
-            span(0, [(i, 1, 1), (i + 1, 1, 1)])
+        with tc.manual_schedule(engines={ENG.DVE}):
+            w_inter(1, 0)
+            span(0, [(0, 0, 1), (1, 0, 1)])
+            w_quant(1, 0)
+            span(0, [(2, 0, 1), (3, 0, 1)])
+            w_inter(1, 1)
+            span(0, [(0, 1, 0), (1, 1, 0)])
+            w_quant(1, 1)
+            span(0, [(2, 1, 0), (3, 1, 0)])
+            x_cast(4)
+            x_transpose(4)
+            x_evac(4)
+            load_x(2, 2, 0, NT * M)
+            x_inter(4)
+            span(0, [(0, 1, 1), (1, 1, 1)])
+            x_quant(4)
+            span(0, [(2, 1, 1), (3, 1, 1)])
+            x_cast(5)
+            x_transpose(5)
+            x_evac(5)
+
         load_x(3, 3, 0, NT * M)
         last = len(SETS) - 1
-        for s in range(3, len(SETS)):
+        for s in range(NT, len(SETS)):
             b, i0, n = SETS[s]
             if s + 1 < len(SETS):
                 x_inter(s + 1)
@@ -299,8 +304,8 @@ def tile_multiheadselfattention_pa_kernel(tc, x_bytes, x_scale, w_aq, w_ak, out_
             for ii in range(n):
                 i = i0 + ii
                 if s == last and ii == n - 1:
-                    span(b, [(i, 0, 0), (i, 0, 1)])
-                    span(b, [(i, 1, 0)])
+                    span(b, [(i, 0, 0), (i, 0, 1)], add_on_vector=True)
+                    span(b, [(i, 1, 0)], add_on_vector=True)
                     span(b, [(i, 1, 1)], add_on_vector=True)
                 elif s == last:
                     span(b, [(i, 0, 0), (i, 0, 1)])

@@ -29,7 +29,7 @@ TWO_PI = 2.0 * PI
 
 SETS = [(0, i, 1) for i in range(NT)] + [(b, i0, 2) for b in range(1, B) for i0 in (0, 2)]
 X_CAST_ON_VECTOR = (1, 2, 3)
-X_INTER_ON_GPSIMD = (0, 1, 2, 3)
+X_INTER_ON_VECTOR = (0, 1, 2, 3)
 W_INTER_ON_VECTOR = ((0, 0, 0), (0, 0, 1), (0, 1, 1))
 
 
@@ -132,9 +132,8 @@ def tile_multiheadselfattention_pa_kernel(tc, x_bytes, x_scale, w_aq, w_ak, out_
             xg = xg_pool.tile([P, G, R, 4], BF16, name="xg", tag="xg", align_bytes=64)
             for g in range(G):
                 src = xp[:, g].rearrange("p t r -> p r t")
-                if s in X_INTER_ON_GPSIMD:
-                    nc.gpsimd.tensor_scalar(out=xg[:, g], in0=src, scalar1=1.0, scalar2=0.0,
-                                            op0=ALU.mult, op1=ALU.add)
+                if s in X_INTER_ON_VECTOR:
+                    nc.vector.tensor_copy(out=xg[:, g], in_=src)
                 else:
                     nc.scalar.copy(out=xg[:, g], in_=src)
             xg_of[s] = xg
@@ -252,14 +251,16 @@ def tile_multiheadselfattention_pa_kernel(tc, x_bytes, x_scale, w_aq, w_ak, out_
             x_transpose(3)
             x_evac(2)
             x_evac(3)
-            for s in range(NT):
-                x_inter(s)
             w_inter(0, 0)
-            x_quant(0)
+            x_inter(0)
             w_quant(0, 0)
-            x_quant(1)
+            x_quant(0)
+            x_inter(1)
             w_inter(0, 1)
+            x_quant(1)
             span(0, [(0, 0, 0)])
+            x_inter(2)
+            x_inter(3)
             x_quant(2)
             span(0, [(1, 0, 0)])
             x_quant(3)

@@ -258,13 +258,13 @@ def tile_multiheadselfattention_pa_kernel(tc, x_bytes, x_scale, w_aq, w_ak, out_
             x_inter(1)
             w_inter(0, 1)
             x_quant(1)
-            span(0, [(0, 0, 0)])
             x_inter(2)
             x_inter(3)
             x_quant(2)
-            span(0, [(1, 0, 0)])
             x_quant(3)
             w_quant(0, 1)
+            span(0, [(0, 0, 0)])
+            span(0, [(1, 0, 0)])
             span(0, [(2, 0, 0), (3, 0, 0)])
 
         load_w(1, 0)
@@ -293,23 +293,25 @@ def tile_multiheadselfattention_pa_kernel(tc, x_bytes, x_scale, w_aq, w_ak, out_
 
         load_x(3, 3, 0, NT * M)
         last = len(SETS) - 1
-        for s in range(NT, len(SETS)):
-            b, i0, n = SETS[s]
-            if s + 1 < len(SETS):
-                x_inter(s + 1)
-                x_quant(s + 1)
-            if s + 2 < len(SETS):
-                x_cast(s + 2)
-                x_transpose(s + 2)
-                x_evac(s + 2)
-            for ii in range(n):
-                i = i0 + ii
-                if s == last and ii == n - 1:
-                    span(b, [(i, 0, 0), (i, 0, 1)], add_on_vector=True)
-                    span(b, [(i, 1, 0)], add_on_vector=True)
-                    span(b, [(i, 1, 1)], add_on_vector=True)
-                elif s == last:
-                    span(b, [(i, 0, 0), (i, 0, 1)])
-                    span(b, [(i, 1, 0), (i, 1, 1)])
-                else:
-                    span(b, [(i, 0, 0), (i, 0, 1), (i, 1, 0), (i, 1, 1)])
+        with tc.manual_schedule(engines={ENG.DVE}):
+            for s in range(NT, len(SETS)):
+                b, i0, n = SETS[s]
+                if s + 1 < len(SETS):
+                    x_inter(s + 1)
+                if s + 2 < len(SETS):
+                    x_cast(s + 2)
+                    x_transpose(s + 2)
+                    x_evac(s + 2)
+                for ii in range(n):
+                    i = i0 + ii
+                    if ii == n - 1 and s + 1 < len(SETS):
+                        x_quant(s + 1)
+                    if s == last and ii == n - 1:
+                        span(b, [(i, 0, 0), (i, 0, 1)], add_on_vector=True)
+                        span(b, [(i, 1, 0)], add_on_vector=True)
+                        span(b, [(i, 1, 1)], add_on_vector=True)
+                    elif s == last:
+                        span(b, [(i, 0, 0), (i, 0, 1)])
+                        span(b, [(i, 1, 0), (i, 1, 1)])
+                    else:
+                        span(b, [(i, 0, 0), (i, 0, 1), (i, 1, 0), (i, 1, 1)])

@@ -131,11 +131,12 @@ def tile_multiheadselfattention_pa_kernel(tc, x_bytes, x_scale, w_aq, w_ak, out_
             xp = xp_of[s]
             xg = xg_pool.tile([P, G, R, 4], BF16, name="xg", tag="xg", align_bytes=64)
             for g in range(G):
-                src = xp[:, g].rearrange("p t r -> p r t")
+                src = xp[:, g].rearrange("p t (c i) -> p c t i", i=4)
+                dst = xg[:, g].rearrange("p (c i) t -> p c t i", i=4)
                 if s in X_INTER_ON_VECTOR:
-                    nc.vector.tensor_copy(out=xg[:, g], in_=src)
+                    nc.vector.tensor_copy(out=dst, in_=src)
                 else:
-                    nc.scalar.copy(out=xg[:, g], in_=src)
+                    nc.scalar.copy(out=dst, in_=src)
             xg_of[s] = xg
 
         def x_quant(s):
@@ -155,11 +156,12 @@ def tile_multiheadselfattention_pa_kernel(tc, x_bytes, x_scale, w_aq, w_ak, out_
         def w_inter(m, c):
             wg = wg_pool.tile([P, G, CH, 4], BF16, name="wg", tag="wg", align_bytes=64)
             for g in range(G):
-                src = wr[(m, g, c)][:].rearrange("p j n -> p n j")
+                src = wr[(m, g, c)][:].rearrange("p j (a i) -> p a j i", i=4)
+                dst = wg[:, g].rearrange("p (a i) j -> p a j i", i=4)
                 if (m, c, g) in W_INTER_ON_VECTOR:
-                    nc.vector.tensor_copy(out=wg[:, g], in_=src)
+                    nc.vector.tensor_copy(out=dst, in_=src)
                 else:
-                    nc.scalar.copy(out=wg[:, g], in_=src)
+                    nc.scalar.copy(out=dst, in_=src)
             wg_of[(m, c)] = wg
 
         def w_quant(m, c):

@@ -28,9 +28,9 @@ PI = 3.141592653589793
 TWO_PI = 2.0 * PI
 
 SETS = [(0, i, 1) for i in range(NT)] + [(b, i0, 2) for b in range(1, B) for i0 in (0, 2)]
-X_CAST_ON_VECTOR = (1, 2, 3)
-X_INTER_ON_VECTOR = (0, 1, 2, 3)
-W_INTER_ON_VECTOR = ((0, 0, 0), (0, 0, 1), (0, 1, 1))
+X_CAST_ON_VECTOR = ()
+X_INTER_ON_VECTOR = ()
+W_INTER_ON_VECTOR = ((0, 0, 0), (0, 0, 1))
 
 
 def tile_multiheadselfattention_pa_kernel(tc, x_bytes, x_scale, w_aq, w_ak, out_0, out_1):
@@ -125,6 +125,16 @@ def tile_multiheadselfattention_pa_kernel(tc, x_bytes, x_scale, w_aq, w_ak, out_
                                          scale=xs[:, g, t:t + 1])
             xp_of[s] = xp
 
+        def x_evac_inter(s):
+            pairs = xbank_of[s][0][:].bitcast(BF16)
+            xg = xg_pool.tile([P, G, P, 4], BF16, name="xg", tag="xg", align_bytes=64)
+            for g in range(G):
+                nc.vector.tensor_tensor(out=xg[:, g].rearrange("p r (u e) -> p r u e", e=2),
+                                        in0=pairs[:, g * 4 * P:(g + 1) * 4 * P].rearrange("p (u r e) -> p r u e", u=2, e=2),
+                                        in1=xs[:, g, :].rearrange("p (u e) -> p u e", e=2).unsqueeze(1).to_broadcast([P, P, 2, 2]),
+                                        op=ALU.mult)
+            xg_of[s] = xg
+
         def x_inter(s):
             b, i0, n = SETS[s]
             R = n * P
@@ -172,7 +182,7 @@ def tile_multiheadselfattention_pa_kernel(tc, x_bytes, x_scale, w_aq, w_ak, out_
                                   in_=wg_of[(m, c)][:].rearrange("p g n j -> p (g n j)"))
             wc_of[(m, c)] = (wc, wsc)
 
-        def span(b, banks, add_on_vector=False):
+        def products(b, banks):
             nh = 4 * len(banks)
             xy = xy_pool.tile([P, nh, 2, D], F32, name="xy", tag="xy")
             for k, (i, m, c) in enumerate(banks):
@@ -188,6 +198,10 @@ def tile_multiheadselfattention_pa_kernel(tc, x_bytes, x_scale, w_aq, w_ak, out_
                                         in0=acc[:].rearrange("p (a j) -> p a j", j=HALF).unsqueeze(2).to_broadcast([P, 8, 2, HALF]),
                                         in1=tab[:, i].rearrange("p q d -> p (q d)").unsqueeze(1).to_broadcast([P, 4, 2 * D]),
                                         op=ALU.mult)
+            return xy
+
+        def add_store(b, banks, xy, add_on_vector=False):
+            nh = 4 * len(banks)
             o = o_pool.tile([P, nh * D], F32, name="o", tag="o")
             eng = nc.vector if add_on_vector else nc.gpsimd
             eng.tensor_tensor(out=o[:].rearrange("p (h d) -> p h d", d=D),
@@ -200,6 +214,9 @@ def tile_multiheadselfattention_pa_kernel(tc, x_bytes, x_scale, w_aq, w_ak, out_
                     n += 1
                 nc.sync.dma_start(out=ov[m][b, i][:, c * CH:(c + n) * CH], in_=o[:, k * CH:(k + n) * CH])
                 k += n
+
+        def span(b, banks):
+            add_store(b, banks, products(b, banks))
 
         ident = const.tile([P, P], F32, name="ident")
         warm = const.tile([P, 1], F32, name="warm")
@@ -236,9 +253,11 @@ def tile_multiheadselfattention_pa_kernel(tc, x_bytes, x_scale, w_aq, w_ak, out_
             nc.scalar.activation(out=sh[:], in_=red[:], func=ACT.Sin, scale=0.5)
             nc.scalar.activation(out=chh[:], in_=hc[:], func=ACT.Sin)
             x_transpose(0)
-            x_cast(1)
-            x_cast(2)
-            x_cast(3)
+            for s in range(1, NT):
+                x_cast(s)
+                x_transpose(s)
+            w_inter(0, 1)
+            x_evac_inter(0)
             nc.vector.scalar_tensor_tensor(out=sq[:], in0=sh[:], scalar=-2.0, in1=sh[:], op0=ALU.mult, op1=ALU.mult)
             nc.vector.tensor_scalar(out=tab[:, :, 0, 0:HALF], in0=sq[:], scalar1=1.0, scalar2=None, op0=ALU.add)
             nc.vector.tensor_scalar(out=tab[:, :, 1, HALF:D], in0=sq[:], scalar1=1.0, scalar2=None, op0=ALU.add)
@@ -246,25 +265,16 @@ def tile_multiheadselfattention_pa_kernel(tc, x_bytes, x_scale, w_aq, w_ak, out_
                                            op0=ALU.mult, op1=ALU.mult)
             nc.vector.scalar_tensor_tensor(out=tab[:, :, 1, 0:HALF], in0=sh[:], scalar=-2.0, in1=chh[:],
                                            op0=ALU.mult, op1=ALU.mult)
-            x_transpose(1)
-            x_evac(0)
-            x_transpose(2)
-            x_evac(1)
-            x_transpose(3)
-            x_evac(2)
-            x_evac(3)
             w_inter(0, 0)
-            x_inter(0)
+            x_evac_inter(1)
             w_quant(0, 0)
             x_quant(0)
-            x_inter(1)
-            w_inter(0, 1)
+            x_evac_inter(2)
             x_quant(1)
-            x_inter(2)
-            x_inter(3)
+            x_evac_inter(3)
             x_quant(2)
-            x_quant(3)
             w_quant(0, 1)
+            x_quant(3)
             span(0, [(0, 0, 0)])
             span(0, [(1, 0, 0)])
             span(0, [(2, 0, 0), (3, 0, 0)])
@@ -309,9 +319,10 @@ def tile_multiheadselfattention_pa_kernel(tc, x_bytes, x_scale, w_aq, w_ak, out_
                     if ii == n - 1 and s + 1 < len(SETS):
                         x_quant(s + 1)
                     if s == last and ii == n - 1:
-                        span(b, [(i, 0, 0), (i, 0, 1)], add_on_vector=True)
-                        span(b, [(i, 1, 0)], add_on_vector=True)
-                        span(b, [(i, 1, 1)], add_on_vector=True)
+                        groups = ([(i, 0, 0), (i, 0, 1)], [(i, 1, 0)], [(i, 1, 1)])
+                        made = [products(b, banks) for banks in groups]
+                        for banks, xy in zip(groups, made):
+                            add_store(b, banks, xy, add_on_vector=True)
                     elif s == last:
                         span(b, [(i, 0, 0), (i, 0, 1)])
                         span(b, [(i, 1, 0), (i, 1, 1)])

@@ -127,13 +127,15 @@ def tile_multiheadselfattention_pa_kernel(tc, x_bytes, x_scale, w_aq, w_ak, out_
 
         def x_evac_inter(s):
             pairs = xbank_of[s][0][:].bitcast(BF16)
-            xg = xg_pool.tile([P, G, P, 4], BF16, name="xg", tag="xg", align_bytes=64)
+            if s % 2 == 0:
+                xg_of[s] = xg_pool.tile([P, G, 2 * P, 4], BF16, name="xg", tag="xg", align_bytes=64)
+            xg = xg_of[s - s % 2]
+            lo = (s % 2) * P
             for g in range(G):
-                nc.vector.tensor_tensor(out=xg[:, g].rearrange("p r (u e) -> p r u e", e=2),
+                nc.vector.tensor_tensor(out=xg[:, g, lo:lo + P].rearrange("p r (u e) -> p r u e", e=2),
                                         in0=pairs[:, g * 4 * P:(g + 1) * 4 * P].rearrange("p (u r e) -> p r u e", u=2, e=2),
                                         in1=xs[:, g, :].rearrange("p (u e) -> p u e", e=2).unsqueeze(1).to_broadcast([P, P, 2, 2]),
                                         op=ALU.mult)
-            xg_of[s] = xg
 
         def x_inter(s):
             b, i0, n = SETS[s]
@@ -149,8 +151,9 @@ def tile_multiheadselfattention_pa_kernel(tc, x_bytes, x_scale, w_aq, w_ak, out_
                     nc.scalar.copy(out=dst, in_=src)
             xg_of[s] = xg
 
-        def x_quant(s):
+        def x_quant(s, n_sets=1):
             b, i0, n = SETS[s]
+            n = n * n_sets
             R = n * P
             xc = const.tile([P, G, R], U32, name="xc%d" % s, align_bytes=64)
             xsc = const.tile([P, G, R], U8, name="xsc%d" % s, align_bytes=64)
@@ -220,7 +223,6 @@ def tile_multiheadselfattention_pa_kernel(tc, x_bytes, x_scale, w_aq, w_ak, out_
 
         ident = const.tile([P, P], F32, name="ident")
         warm = const.tile([P, 1], F32, name="warm")
-        pos = const.tile([P, NT, 1], I32, name="pos")
         ang = const.tile([P, NT, HALF], F32, name="ang")
         turns = const.tile([P, NT, HALF], I32, name="turns")
         red = const.tile([P, NT, HALF], F32, name="red")
@@ -232,11 +234,11 @@ def tile_multiheadselfattention_pa_kernel(tc, x_bytes, x_scale, w_aq, w_ak, out_
         tab = const.tile([P, NT, 2, D], F32, name="tab")
 
         with tc.manual_schedule(engines={ENG.PE, ENG.DVE, ENG.Activation, ENG.Pool}):
-            nc.gpsimd.iota(pos[:], pattern=[[1, NT]], base=0, channel_multiplier=NT)
+            nc.gpsimd.iota(ang[:, :, 0:1], pattern=[[1, NT]], base=0, channel_multiplier=NT,
+                           allow_small_or_imprecise_dtypes=True)
             make_identity(nc, ident[:])
             nc.vector.memset(warm[:], 0.0)
             nc.scalar.activation(out=warm[:], in_=warm[:], func=ACT.Sin)
-            nc.vector.tensor_copy(out=ang[:, :, 0:1], in_=pos[:])
             for k in range(6):
                 w = 2 ** k
                 nc.vector.tensor_scalar(out=ang[:, :, w:2 * w], in0=ang[:, :, 0:w], scalar1=RATIO ** w,
@@ -259,8 +261,9 @@ def tile_multiheadselfattention_pa_kernel(tc, x_bytes, x_scale, w_aq, w_ak, out_
             w_inter(0, 1)
             x_evac_inter(0)
             nc.vector.scalar_tensor_tensor(out=sq[:], in0=sh[:], scalar=-2.0, in1=sh[:], op0=ALU.mult, op1=ALU.mult)
-            nc.vector.tensor_scalar(out=tab[:, :, 0, 0:HALF], in0=sq[:], scalar1=1.0, scalar2=None, op0=ALU.add)
-            nc.vector.tensor_scalar(out=tab[:, :, 1, HALF:D], in0=sq[:], scalar1=1.0, scalar2=None, op0=ALU.add)
+            nc.vector.tensor_scalar(out=tab[:].rearrange("p i q (a j) -> p i (q a) j", j=HALF)[:, :, 0:4:3, :],
+                                    in0=sq[:].unsqueeze(2).to_broadcast([P, NT, 2, HALF]), scalar1=1.0, scalar2=None,
+                                    op0=ALU.add)
             nc.vector.scalar_tensor_tensor(out=tab[:, :, 0, HALF:D], in0=sh[:], scalar=2.0, in1=chh[:],
                                            op0=ALU.mult, op1=ALU.mult)
             nc.vector.scalar_tensor_tensor(out=tab[:, :, 1, 0:HALF], in0=sh[:], scalar=-2.0, in1=chh[:],
@@ -268,13 +271,11 @@ def tile_multiheadselfattention_pa_kernel(tc, x_bytes, x_scale, w_aq, w_ak, out_
             w_inter(0, 0)
             x_evac_inter(1)
             w_quant(0, 0)
-            x_quant(0)
+            x_quant(0, n_sets=2)
             x_evac_inter(2)
-            x_quant(1)
             x_evac_inter(3)
-            x_quant(2)
             w_quant(0, 1)
-            x_quant(3)
+            x_quant(2, n_sets=2)
             span(0, [(0, 0, 0)])
             span(0, [(1, 0, 0)])
             span(0, [(2, 0, 0), (3, 0, 0)])

@@ -28,9 +28,8 @@ PI = 3.141592653589793
 TWO_PI = 2.0 * PI
 
 SETS = [(0, i, 1) for i in range(NT)] + [(b, i0, 2) for b in range(1, B) for i0 in (0, 2)]
-X_CAST_ON_VECTOR = ()
 X_INTER_ON_VECTOR = ()
-W_INTER_ON_VECTOR = ((0, 0, 0), (0, 0, 1))
+W_INTER_ON_GPSIMD = ((0, 0, 0),)
 
 
 def tile_multiheadselfattention_pa_kernel(tc, x_bytes, x_scale, w_aq, w_ak, out_0, out_1):
@@ -59,8 +58,8 @@ def tile_multiheadselfattention_pa_kernel(tc, x_bytes, x_scale, w_aq, w_ak, out_
             xb_of[key] = xb_pool.tile([P, hi - lo], U8, name="xbytes", tag="xbytes")
             nc.sync.dma_start(out=xb_of[key][:], in_=xv[b][:, lo:hi])
 
-        def load_w(m, c):
-            for g in range(G):
+        def load_w(m, c, passes=(0, 1)):
+            for g in passes:
                 wr[(m, g, c)] = wr_pool.tile([P, 4, CH], BF16, name="wr", tag="wr")
                 nc.sync.dma_start(out=wr[(m, g, c)][:], in_=wv[m][g][:, :, c * CH:(c + 1) * CH])
 
@@ -74,8 +73,9 @@ def tile_multiheadselfattention_pa_kernel(tc, x_bytes, x_scale, w_aq, w_ak, out_
         xs = const.tile([P, G, 4], F32, name="xs")
         load_x("a", 0, 0, M)
         nc.sync.dma_start(out=xs[:], in_=x_scale[0, 0, :].rearrange("(g p t) -> p g t", g=G, p=P, t=4))
+        load_w(0, 0, (0,))
         load_x("b", 0, M, NT * M)
-        load_w(0, 0)
+        load_w(0, 0, (1,))
         load_w(0, 1)
 
         xw_of = {}
@@ -87,10 +87,10 @@ def tile_multiheadselfattention_pa_kernel(tc, x_bytes, x_scale, w_aq, w_ak, out_
         def x_cast(s):
             b, i0, n = SETS[s]
             xw_of[s] = xw_pool.tile([P, n * M], BF16, name="xw", tag="xw")
-            if s in X_CAST_ON_VECTOR:
-                nc.vector.tensor_copy(out=xw_of[s][:], in_=bytes_of(b, i0, n).bitcast(FP8))
-            else:
-                nc.scalar.copy(out=xw_of[s][:], in_=bytes_of(b, i0, n).bitcast(FP8))
+            parts = 2 if s == 0 else 1
+            w = n * M // parts
+            for k in range(parts):
+                nc.scalar.copy(out=xw_of[s][:, k * w:(k + 1) * w], in_=bytes_of(b, i0, n)[:, k * w:(k + 1) * w].bitcast(FP8))
 
         def x_transpose(s):
             b, i0, n = SETS[s]
@@ -171,8 +171,8 @@ def tile_multiheadselfattention_pa_kernel(tc, x_bytes, x_scale, w_aq, w_ak, out_
             for g in range(G):
                 src = wr[(m, g, c)][:].rearrange("p j (a i) -> p a j i", i=4)
                 dst = wg[:, g].rearrange("p (a i) j -> p a j i", i=4)
-                if (m, c, g) in W_INTER_ON_VECTOR:
-                    nc.vector.tensor_copy(out=dst, in_=src)
+                if (m, c, g) in W_INTER_ON_GPSIMD:
+                    nc.gpsimd.tensor_scalar(out=dst, in0=src, scalar1=1.0, scalar2=0.0, op0=ALU.mult, op1=ALU.add)
                 else:
                     nc.scalar.copy(out=dst, in_=src)
             wg_of[(m, c)] = wg
@@ -252,13 +252,14 @@ def tile_multiheadselfattention_pa_kernel(tc, x_bytes, x_scale, w_aq, w_ak, out_
             nc.vector.tensor_scalar(out=hc[:], in0=mag[:], scalar1=-0.5, scalar2=0.5 * PI,
                                     op0=ALU.mult, op1=ALU.add)
             x_cast(0)
+            x_transpose(0)
             nc.scalar.activation(out=sh[:], in_=red[:], func=ACT.Sin, scale=0.5)
             nc.scalar.activation(out=chh[:], in_=hc[:], func=ACT.Sin)
-            x_transpose(0)
-            for s in range(1, NT):
-                x_cast(s)
-                x_transpose(s)
-            w_inter(0, 1)
+            x_cast(1)
+            x_transpose(1)
+            w_inter(0, 0)
+            x_cast(2)
+            x_transpose(2)
             x_evac_inter(0)
             nc.vector.scalar_tensor_tensor(out=sq[:], in0=sh[:], scalar=-2.0, in1=sh[:], op0=ALU.mult, op1=ALU.mult)
             nc.vector.tensor_scalar(out=tab[:].rearrange("p i q (a j) -> p i (q a) j", j=HALF)[:, :, 0:4:3, :],
@@ -268,17 +269,21 @@ def tile_multiheadselfattention_pa_kernel(tc, x_bytes, x_scale, w_aq, w_ak, out_
                                            op0=ALU.mult, op1=ALU.mult)
             nc.vector.scalar_tensor_tensor(out=tab[:, :, 1, 0:HALF], in0=sh[:], scalar=-2.0, in1=chh[:],
                                            op0=ALU.mult, op1=ALU.mult)
-            w_inter(0, 0)
             x_evac_inter(1)
             w_quant(0, 0)
             x_quant(0, n_sets=2)
             x_evac_inter(2)
+            x_cast(3)
+            w_inter(0, 1)
+            xy0 = products(0, [(0, 0, 0)])
+            x_transpose(3)
+            add_store(0, [(0, 0, 0)], xy0)
             x_evac_inter(3)
-            w_quant(0, 1)
             x_quant(2, n_sets=2)
-            span(0, [(0, 0, 0)])
             span(0, [(1, 0, 0)])
-            span(0, [(2, 0, 0), (3, 0, 0)])
+            span(0, [(2, 0, 0)])
+            w_quant(0, 1)
+            span(0, [(3, 0, 0)])
 
         load_w(1, 0)
         load_x(1, 1, 0, NT * M)

@@ -172,7 +172,8 @@ def tile_multiheadselfattention_pa_kernel(tc, x_bytes, x_scale, w_aq, w_ak, out_
                 src = wr[(m, g, c)][:].rearrange("p j (a i) -> p a j i", i=4)
                 dst = wg[:, g].rearrange("p (a i) j -> p a j i", i=4)
                 if (m, c, g) in W_INTER_ON_GPSIMD:
-                    nc.gpsimd.tensor_scalar(out=dst, in0=src, scalar1=1.0, scalar2=0.0, op0=ALU.mult, op1=ALU.add)
+                    nc.gpsimd.tensor_scalar(out=wg[:, g], in0=wr[(m, g, c)][:].rearrange("p j n -> p n j"),
+                                            scalar1=1.0, scalar2=0.0, op0=ALU.mult, op1=ALU.add)
                 else:
                     nc.scalar.copy(out=dst, in_=src)
             wg_of[(m, c)] = wg

@@ -43,6 +43,7 @@ def tile_multiheadselfattention_pa_kernel(tc, x_bytes, x_scale, w_aq, w_ak, out_
         xg_pool = ctx.enter_context(tc.tile_pool(name="xg", bufs=3))
         wg_pool = ctx.enter_context(tc.tile_pool(name="wg", bufs=2))
         xy_pool = ctx.enter_context(tc.tile_pool(name="xy", bufs=4))
+        x3_pool = ctx.enter_context(tc.tile_pool(name="x3", bufs=2))
         o_pool = ctx.enter_context(tc.tile_pool(name="o", bufs=5))
         psx = ctx.enter_context(tc.psum_pool(name="psx", bufs=3))
         psu = ctx.enter_context(tc.psum_pool(name="psu", bufs=5))
@@ -126,15 +127,19 @@ def tile_multiheadselfattention_pa_kernel(tc, x_bytes, x_scale, w_aq, w_ak, out_
             xp_of[s] = xp
 
         def x_evac_inter(s):
-            pairs = xbank_of[s][0][:].bitcast(BF16)
-            if s % 2 == 0:
+            b, i0, n = SETS[s]
+            R = n * P
+            if b > 0 or s % 2 == 0:
                 xg_of[s] = xg_pool.tile([P, G, 2 * P, 4], BF16, name="xg", tag="xg", align_bytes=64)
-            xg = xg_of[s - s % 2]
-            lo = (s % 2) * P
+            xg, lo = (xg_of[s], 0) if b > 0 else (xg_of[s - s % 2], (s % 2) * P)
             for g in range(G):
-                nc.vector.tensor_tensor(out=xg[:, g, lo:lo + P].rearrange("p r (u e) -> p r u e", e=2),
-                                        in0=pairs[:, g * 4 * P:(g + 1) * 4 * P].rearrange("p (u r e) -> p r u e", u=2, e=2),
-                                        in1=xs[:, g, :].rearrange("p (u e) -> p u e", e=2).unsqueeze(1).to_broadcast([P, P, 2, 2]),
+                if n == 1:
+                    words = xbank_of[s][0][:, g * 2 * R:(g + 1) * 2 * R]
+                else:
+                    words = xbank_of[s][g][:]
+                nc.vector.tensor_tensor(out=xg[:, g, lo:lo + R].rearrange("p r (u e) -> p r u e", e=2),
+                                        in0=words.bitcast(BF16).rearrange("p (u r e) -> p r u e", u=2, e=2),
+                                        in1=xs[:, g, :].rearrange("p (u e) -> p u e", e=2).unsqueeze(1).to_broadcast([P, R, 2, 2]),
                                         op=ALU.mult)
 
         def x_inter(s):
@@ -169,13 +174,15 @@ def tile_multiheadselfattention_pa_kernel(tc, x_bytes, x_scale, w_aq, w_ak, out_
         def w_inter(m, c):
             wg = wg_pool.tile([P, G, CH, 4], BF16, name="wg", tag="wg", align_bytes=64)
             for g in range(G):
-                src = wr[(m, g, c)][:].rearrange("p j (a i) -> p a j i", i=4)
-                dst = wg[:, g].rearrange("p (a i) j -> p a j i", i=4)
-                if (m, c, g) in W_INTER_ON_GPSIMD:
-                    nc.gpsimd.tensor_scalar(out=wg[:, g], in0=wr[(m, g, c)][:].rearrange("p j n -> p n j"),
-                                            scalar1=1.0, scalar2=0.0, op0=ALU.mult, op1=ALU.add)
-                else:
-                    nc.scalar.copy(out=dst, in_=src)
+                for f in range(2):
+                    src = wr[(m, g, c)][:].rearrange("p j (h f a i) -> p f h a j i", f=2, a=HALF // 4, i=4)[:, 1 - f]
+                    dst = wg[:, g].rearrange("p (f h a i) j -> p f h a j i", f=2, a=HALF // 4, i=4)[:, f]
+                    if (m, c, g) in W_INTER_ON_GPSIMD:
+                        nc.gpsimd.tensor_scalar(out=wg[:, g, f * 256:(f + 1) * 256].rearrange("p (h e) j -> p h e j", e=HALF),
+                                                in0=wr[(m, g, c)][:].rearrange("p j (h f e) -> p f h e j", f=2, e=HALF)[:, 1 - f],
+                                                scalar1=1.0, scalar2=0.0, op0=ALU.mult, op1=ALU.add)
+                    else:
+                        nc.scalar.copy(out=dst, in_=src)
             wg_of[(m, c)] = wg
 
         def w_quant(m, c):
@@ -186,30 +193,39 @@ def tile_multiheadselfattention_pa_kernel(tc, x_bytes, x_scale, w_aq, w_ak, out_
                                   in_=wg_of[(m, c)][:].rearrange("p g n j -> p (g n j)"))
             wc_of[(m, c)] = (wc, wsc)
 
+        def project(b, i, m, c):
+            xc, xsc, off = xc_of[(b, i)]
+            wc, wsc = wc_of[(m, c)]
+            acc = psu.tile([P, CH], F32, name="acc", tag="acc")
+            for g in range(G):
+                nc.tensor.matmul_mx(out=acc[:],
+                                    lhsT=xc[:, g, off:off + P].bitcast(FP8X4), lhsT_scale=xsc[:, g, off:off + P],
+                                    rhs=wc[:, g, :].bitcast(FP8X4), rhs_scale=wsc[:, g, :],
+                                    start=(g == 0), stop=(g == G - 1))
+            return acc
+
+        def half_sums(b, i, m, c, out):
+            xc, xsc, off = xc_of[(b, i)]
+            wc, wsc = wc_of[(m, c)]
+            for k in range(2 * G):
+                g, f = k // 2, k % 2
+                nc.tensor.matmul_mx(out=out,
+                                    lhsT=xc[:, g, off:off + P].bitcast(FP8X4), lhsT_scale=xsc[:, g, off:off + P],
+                                    rhs=wc[:, g, f * 256:(f + 1) * 256].bitcast(FP8X4),
+                                    rhs_scale=wsc[:, g, f * 256:(f + 1) * 256],
+                                    start=(k == 0), stop=(k == 2 * G - 1))
+
         def products(b, banks):
-            nh = 4 * len(banks)
-            xy = xy_pool.tile([P, nh, 2, D], F32, name="xy", tag="xy")
+            xy = xy_pool.tile([P, len(banks), 2, CH], F32, name="xy", tag="xy")
             for k, (i, m, c) in enumerate(banks):
-                xc, xsc, off = xc_of[(b, i)]
-                wc, wsc = wc_of[(m, c)]
-                acc = psu.tile([P, CH], F32, name="acc", tag="acc")
-                for g in range(G):
-                    nc.tensor.matmul_mx(out=acc[:],
-                                        lhsT=xc[:, g, off:off + P].bitcast(FP8X4), lhsT_scale=xsc[:, g, off:off + P],
-                                        rhs=wc[:, g, :].bitcast(FP8X4), rhs_scale=wsc[:, g, :],
-                                        start=(g == 0), stop=(g == G - 1))
-                nc.vector.tensor_tensor(out=xy[:, 4 * k:4 * k + 4].rearrange("p h q d -> p (h q d)"),
-                                        in0=acc[:].rearrange("p (a j) -> p a j", j=HALF).unsqueeze(2).to_broadcast([P, 8, 2, HALF]),
-                                        in1=tab[:, i].rearrange("p q d -> p (q d)").unsqueeze(1).to_broadcast([P, 4, 2 * D]),
+                acc = project(b, i, m, c)
+                nc.vector.tensor_tensor(out=xy[:, k].rearrange("p q n -> p (q n)"),
+                                        in0=acc[:].rearrange("p (a e) -> p a e", e=HALF).unsqueeze(2).to_broadcast([P, 8, 2, HALF]),
+                                        in1=tab[:, i].unsqueeze(2).to_broadcast([P, 2, 4, D]),
                                         op=ALU.mult)
             return xy
 
-        def add_store(b, banks, xy, add_on_vector=False):
-            nh = 4 * len(banks)
-            o = o_pool.tile([P, nh * D], F32, name="o", tag="o")
-            eng = nc.vector if add_on_vector else nc.gpsimd
-            eng.tensor_tensor(out=o[:].rearrange("p (h d) -> p h d", d=D),
-                              in0=xy[:, :, 0, :], in1=xy[:, :, 1, :], op=ALU.add)
+        def store(b, banks, o):
             k = 0
             while k < len(banks):
                 i, m, c = banks[k]
@@ -219,8 +235,53 @@ def tile_multiheadselfattention_pa_kernel(tc, x_bytes, x_scale, w_aq, w_ak, out_
                 nc.sync.dma_start(out=ov[m][b, i][:, c * CH:(c + n) * CH], in_=o[:, k * CH:(k + n) * CH])
                 k += n
 
+        def add_store(b, banks, xy, add_on_vector=False):
+            o = o_pool.tile([P, len(banks) * CH], F32, name="o", tag="o")
+            eng = nc.vector if add_on_vector else nc.gpsimd
+            eng.tensor_tensor(out=o[:].rearrange("p (k n) -> p k n", n=CH),
+                              in0=xy[:, :, 0, :], in1=xy[:, :, 1, :], op=ALU.add)
+            store(b, banks, o)
+
         def span(b, banks):
             add_store(b, banks, products(b, banks))
+
+        def products3(b, banks):
+            sums = psu.tile([P, CH], F32, name="acc", tag="acc")
+            k3 = x3_pool.tile([P, 2, 4, HALF], F32, name="k3", tag="k3")
+            kk = x3_pool.tile([P, 2, 4, 2, HALF], F32, name="kk", tag="kk")
+            for k, (i, m, c) in enumerate(banks):
+                acc = project(b, i, m, c)
+                half_sums(b, i, m, c, sums[:, k * 256:(k + 1) * 256])
+                nc.vector.tensor_tensor(out=kk[:, k].rearrange("p h q e -> p q h e"),
+                                        in0=acc[:].rearrange("p (q h e) -> p q h e", q=2, e=HALF),
+                                        in1=tab3[:, i].unsqueeze(2).to_broadcast([P, 2, 4, HALF]),
+                                        op=ALU.mult)
+            i0, i1 = banks[0][0], banks[1][0]
+            cos = tab[:, i0:i1 + 1, 0, HALF:D]
+            if i0 == i1:
+                cos = cos.to_broadcast([P, 2, HALF])
+            nc.vector.tensor_tensor(out=k3[:], in0=sums[:].rearrange("p (k h e) -> p k h e", k=2, e=HALF),
+                                    in1=cos.unsqueeze(2).to_broadcast([P, 2, 4, HALF]), op=ALU.mult)
+            return k3, kk
+
+        def add_store3(b, banks, k3, kk):
+            o = o_pool.tile([P, 2 * CH], F32, name="o", tag="o")
+            nc.gpsimd.tensor_tensor(out=o[:].rearrange("p (a q e) -> p a q e", q=2, e=HALF),
+                                    in0=k3[:].rearrange("p k h e -> p (k h) e").unsqueeze(2).to_broadcast([P, 8, 2, HALF]),
+                                    in1=kk[:].rearrange("p k h q e -> p (k h) q e"), op=ALU.add)
+            store(b, banks, o)
+
+        def span3(b, banks):
+            add_store3(b, banks, *products3(b, banks))
+
+        def sum_on_tensor(b, banks, xy):
+            o = o_pool.tile([P, len(banks) * CH], F32, name="o", tag="o")
+            for k in range(len(banks)):
+                bank = psx.tile([P, CH], F32, name="xbank", tag="xbank")
+                for q in range(2):
+                    nc.tensor.matmul(bank[:], lhsT=ident[:], rhs=xy[:, k, q, :], start=(q == 0), stop=(q == 1))
+                nc.scalar.copy(out=o[:, k * CH:(k + 1) * CH], in_=bank[:])
+            store(b, banks, o)
 
         ident = const.tile([P, P], F32, name="ident")
         warm = const.tile([P, 1], F32, name="warm")
@@ -233,6 +294,7 @@ def tile_multiheadselfattention_pa_kernel(tc, x_bytes, x_scale, w_aq, w_ak, out_
         chh = const.tile([P, NT, HALF], F32, name="chh")
         sq = const.tile([P, NT, HALF], F32, name="sq")
         tab = const.tile([P, NT, 2, D], F32, name="tab")
+        tab3 = const.tile([P, NT, 2, HALF], F32, name="tab3")
 
         with tc.manual_schedule(engines={ENG.PE, ENG.DVE, ENG.Activation, ENG.Pool}):
             nc.gpsimd.iota(ang[:, :, 0:1], pattern=[[1, NT]], base=0, channel_multiplier=NT,
@@ -263,14 +325,17 @@ def tile_multiheadselfattention_pa_kernel(tc, x_bytes, x_scale, w_aq, w_ak, out_
             x_transpose(2)
             x_evac_inter(0)
             nc.vector.scalar_tensor_tensor(out=sq[:], in0=sh[:], scalar=-2.0, in1=sh[:], op0=ALU.mult, op1=ALU.mult)
-            nc.vector.tensor_scalar(out=tab[:].rearrange("p i q (a j) -> p i (q a) j", j=HALF)[:, :, 0:4:3, :],
+            nc.vector.tensor_scalar(out=tab[:].rearrange("p i q (a j) -> p i (q a) j", j=HALF)[:, :, 1:3, :],
                                     in0=sq[:].unsqueeze(2).to_broadcast([P, NT, 2, HALF]), scalar1=1.0, scalar2=None,
                                     op0=ALU.add)
-            nc.vector.scalar_tensor_tensor(out=tab[:, :, 0, HALF:D], in0=sh[:], scalar=2.0, in1=chh[:],
+            nc.vector.scalar_tensor_tensor(out=tab[:, :, 1, HALF:D], in0=sh[:], scalar=2.0, in1=chh[:],
                                            op0=ALU.mult, op1=ALU.mult)
-            nc.vector.scalar_tensor_tensor(out=tab[:, :, 1, 0:HALF], in0=sh[:], scalar=-2.0, in1=chh[:],
+            nc.vector.scalar_tensor_tensor(out=tab[:, :, 0, 0:HALF], in0=sh[:], scalar=-2.0, in1=chh[:],
                                            op0=ALU.mult, op1=ALU.mult)
             x_evac_inter(1)
+            for q, op in ((0, ALU.subtract), (1, ALU.add)):
+                nc.vector.scalar_tensor_tensor(out=tab3[:, :, q], in0=tab[:, :, 1, 0:HALF], scalar=-1.0,
+                                               in1=tab[:, :, 1, HALF:D], op0=ALU.mult, op1=op)
             w_quant(0, 0)
             x_quant(0, n_sets=2)
             x_evac_inter(2)
@@ -300,9 +365,8 @@ def tile_multiheadselfattention_pa_kernel(tc, x_bytes, x_scale, w_aq, w_ak, out_
             span(0, [(2, 1, 0), (3, 1, 0)])
             x_cast(4)
             x_transpose(4)
-            x_evac(4)
             load_x(2, 2, 0, NT * M)
-            x_inter(4)
+            x_evac_inter(4)
             span(0, [(0, 1, 1), (1, 1, 1)])
             x_quant(4)
             span(0, [(2, 1, 1), (3, 1, 1)])
@@ -321,17 +385,21 @@ def tile_multiheadselfattention_pa_kernel(tc, x_bytes, x_scale, w_aq, w_ak, out_
                     x_cast(s + 2)
                     x_transpose(s + 2)
                     x_evac(s + 2)
-                for ii in range(n):
-                    i = i0 + ii
-                    if ii == n - 1 and s + 1 < len(SETS):
-                        x_quant(s + 1)
-                    if s == last and ii == n - 1:
-                        groups = ([(i, 0, 0), (i, 0, 1)], [(i, 1, 0)], [(i, 1, 1)])
-                        made = [products(b, banks) for banks in groups]
-                        for banks, xy in zip(groups, made):
-                            add_store(b, banks, xy, add_on_vector=True)
-                    elif s == last:
-                        span(b, [(i, 0, 0), (i, 0, 1)])
-                        span(b, [(i, 1, 0), (i, 1, 1)])
-                    else:
-                        span(b, [(i, 0, 0), (i, 0, 1), (i, 1, 0), (i, 1, 1)])
+                i = i0
+                early = [(i, 0, 0), (i, 0, 1), (i, 1, 0)]
+                late = [(i + 1, 0, 0), (i + 1, 0, 1)]
+                if s == last:
+                    span(b, early)
+                    sum_on_tensor(*waiting)
+                    span3(b, [(i, 1, 1), (i + 1, 1, 1)])
+                    made = [products(b, [bank]) for bank in late + [(i + 1, 1, 0)]]
+                    for bank, xy in zip(late + [(i + 1, 1, 0)], made):
+                        add_store(b, [bank], xy, add_on_vector=True)
+                else:
+                    span(b, early)
+                    if s > NT:
+                        sum_on_tensor(*waiting)
+                    x_quant(s + 1)
+                    span3(b, [(i, 1, 1), (i + 1, 1, 1)])
+                    waiting = (b, [(i + 1, 1, 0)], products(b, [(i + 1, 1, 0)]))
+                    span(b, late)

@@ -44,7 +44,7 @@ def tile_multiheadselfattention_pa_kernel(tc, x_bytes, x_scale, w_aq, w_ak, out_
         wg_pool = ctx.enter_context(tc.tile_pool(name="wg", bufs=2))
         xy_pool = ctx.enter_context(tc.tile_pool(name="xy", bufs=4))
         x3_pool = ctx.enter_context(tc.tile_pool(name="x3", bufs=2))
-        o_pool = ctx.enter_context(tc.tile_pool(name="o", bufs=5))
+        o_pool = ctx.enter_context(tc.tile_pool(name="o", bufs=6))
         psx = ctx.enter_context(tc.psum_pool(name="psx", bufs=3))
         psu = ctx.enter_context(tc.psum_pool(name="psu", bufs=5))
 
@@ -264,9 +264,10 @@ def tile_multiheadselfattention_pa_kernel(tc, x_bytes, x_scale, w_aq, w_ak, out_
                                     in1=cos.unsqueeze(2).to_broadcast([P, 2, 4, HALF]), op=ALU.mult)
             return k3, kk
 
-        def add_store3(b, banks, k3, kk):
+        def add_store3(b, banks, k3, kk, add_on_vector=False):
             o = o_pool.tile([P, 2 * CH], F32, name="o", tag="o")
-            nc.gpsimd.tensor_tensor(out=o[:].rearrange("p (a q e) -> p a q e", q=2, e=HALF),
+            eng = nc.vector if add_on_vector else nc.gpsimd
+            eng.tensor_tensor(out=o[:].rearrange("p (a q e) -> p a q e", q=2, e=HALF),
                                     in0=k3[:].rearrange("p k h e -> p (k h) e").unsqueeze(2).to_broadcast([P, 8, 2, HALF]),
                                     in1=kk[:].rearrange("p k h q e -> p (k h) q e"), op=ALU.add)
             store(b, banks, o)
@@ -324,6 +325,7 @@ def tile_multiheadselfattention_pa_kernel(tc, x_bytes, x_scale, w_aq, w_ak, out_
             x_cast(2)
             x_transpose(2)
             x_evac_inter(0)
+            x_evac_inter(1)
             nc.vector.scalar_tensor_tensor(out=sq[:], in0=sh[:], scalar=-2.0, in1=sh[:], op0=ALU.mult, op1=ALU.mult)
             nc.vector.tensor_scalar(out=tab[:].rearrange("p i q (a j) -> p i (q a) j", j=HALF)[:, :, 1:3, :],
                                     in0=sq[:].unsqueeze(2).to_broadcast([P, NT, 2, HALF]), scalar1=1.0, scalar2=None,
@@ -332,7 +334,6 @@ def tile_multiheadselfattention_pa_kernel(tc, x_bytes, x_scale, w_aq, w_ak, out_
                                            op0=ALU.mult, op1=ALU.mult)
             nc.vector.scalar_tensor_tensor(out=tab[:, :, 0, 0:HALF], in0=sh[:], scalar=-2.0, in1=chh[:],
                                            op0=ALU.mult, op1=ALU.mult)
-            x_evac_inter(1)
             for q, op in ((0, ALU.subtract), (1, ALU.add)):
                 nc.vector.scalar_tensor_tensor(out=tab3[:, :, q], in0=tab[:, :, 1, 0:HALF], scalar=-1.0,
                                                in1=tab[:, :, 1, HALF:D], op0=ALU.mult, op1=op)
@@ -367,9 +368,9 @@ def tile_multiheadselfattention_pa_kernel(tc, x_bytes, x_scale, w_aq, w_ak, out_
             x_transpose(4)
             load_x(2, 2, 0, NT * M)
             x_evac_inter(4)
-            span(0, [(0, 1, 1), (1, 1, 1)])
+            span3(0, [(0, 1, 1), (1, 1, 1)])
             x_quant(4)
-            span(0, [(2, 1, 1), (3, 1, 1)])
+            span3(0, [(2, 1, 1), (3, 1, 1)])
             x_cast(5)
             x_transpose(5)
             x_evac(5)
@@ -389,10 +390,12 @@ def tile_multiheadselfattention_pa_kernel(tc, x_bytes, x_scale, w_aq, w_ak, out_
                 early = [(i, 0, 0), (i, 0, 1), (i, 1, 0)]
                 late = [(i + 1, 0, 0), (i + 1, 0, 1)]
                 if s == last:
-                    span(b, early)
-                    sum_on_tensor(*waiting)
                     span3(b, [(i, 1, 1), (i + 1, 1, 1)])
+                    sum_on_tensor(*waiting)
+                    waiting = (b, early[2:], products(b, early[2:]))
+                    span(b, early[:2])
                     made = [products(b, [bank]) for bank in late + [(i + 1, 1, 0)]]
+                    sum_on_tensor(*waiting)
                     for bank, xy in zip(late + [(i + 1, 1, 0)], made):
                         add_store(b, [bank], xy, add_on_vector=True)
                 else:

@@ -29,7 +29,8 @@ TWO_PI = 2.0 * PI
 
 SETS = [(0, i, 1) for i in range(NT)] + [(b, i0, 2) for b in range(1, B) for i0 in (0, 2)]
 X_INTER_ON_VECTOR = ()
-W_INTER_ON_GPSIMD = ((0, 0, 0),)
+W_INTER_ON_GPSIMD = ((0, 0, 0, 0),)
+W_INTER_ON_VECTOR = ((0, 0, 0, 1),)
 
 
 def tile_multiheadselfattention_pa_kernel(tc, x_bytes, x_scale, w_aq, w_ak, out_0, out_1):
@@ -97,7 +98,7 @@ def tile_multiheadselfattention_pa_kernel(tc, x_bytes, x_scale, w_aq, w_ak, out_
             b, i0, n = SETS[s]
             R = n * P
             words = xw_of[s][:].bitcast(F32)
-            per = 4 // n
+            per = 2
             banks = []
             for q in range(4):
                 g, u = q // 2, q % 2
@@ -114,7 +115,7 @@ def tile_multiheadselfattention_pa_kernel(tc, x_bytes, x_scale, w_aq, w_ak, out_
         def x_evac(s):
             b, i0, n = SETS[s]
             R = n * P
-            per = 4 // n
+            per = 2
             xp = xp_pool.tile([P, G, 4, R], BF16, name="xp", tag="xp")
             for q in range(4):
                 g, u = q // 2, q % 2
@@ -129,14 +130,13 @@ def tile_multiheadselfattention_pa_kernel(tc, x_bytes, x_scale, w_aq, w_ak, out_
         def x_evac_inter(s):
             b, i0, n = SETS[s]
             R = n * P
-            if b > 0 or s % 2 == 0:
-                xg_of[s] = xg_pool.tile([P, G, 2 * P, 4], BF16, name="xg", tag="xg", align_bytes=64)
-            xg, lo = (xg_of[s], 0) if b > 0 else (xg_of[s - s % 2], (s % 2) * P)
+            if s == 2:
+                xg_of[2] = xg_of[3] = xg_pool.tile([P, G, 2 * P, 4], BF16, name="xg", tag="xg", align_bytes=64)
+            elif s != 3:
+                xg_of[s] = xg_pool.tile([P, G, R, 4], BF16, name="xg", tag="xg", align_bytes=64)
+            xg, lo = xg_of[s], P if s == 3 else 0
             for g in range(G):
-                if n == 1:
-                    words = xbank_of[s][0][:, g * 2 * R:(g + 1) * 2 * R]
-                else:
-                    words = xbank_of[s][g][:]
+                words = xbank_of[s][g][:, :2 * R]
                 nc.vector.tensor_tensor(out=xg[:, g, lo:lo + R].rearrange("p r (u e) -> p r u e", e=2),
                                         in0=words.bitcast(BF16).rearrange("p (u r e) -> p r u e", u=2, e=2),
                                         in1=xs[:, g, :].rearrange("p (u e) -> p u e", e=2).unsqueeze(1).to_broadcast([P, R, 2, 2]),
@@ -177,10 +177,12 @@ def tile_multiheadselfattention_pa_kernel(tc, x_bytes, x_scale, w_aq, w_ak, out_
                 for f in range(2):
                     src = wr[(m, g, c)][:].rearrange("p j (h f a i) -> p f h a j i", f=2, a=HALF // 4, i=4)[:, 1 - f]
                     dst = wg[:, g].rearrange("p (f h a i) j -> p f h a j i", f=2, a=HALF // 4, i=4)[:, f]
-                    if (m, c, g) in W_INTER_ON_GPSIMD:
+                    if (m, c, g, f) in W_INTER_ON_GPSIMD:
                         nc.gpsimd.tensor_scalar(out=wg[:, g, f * 256:(f + 1) * 256].rearrange("p (h e) j -> p h e j", e=HALF),
                                                 in0=wr[(m, g, c)][:].rearrange("p j (h f e) -> p f h e j", f=2, e=HALF)[:, 1 - f],
                                                 scalar1=1.0, scalar2=0.0, op0=ALU.mult, op1=ALU.add)
+                    elif (m, c, g, f) in W_INTER_ON_VECTOR:
+                        nc.vector.tensor_copy(out=dst, in_=src)
                     else:
                         nc.scalar.copy(out=dst, in_=src)
             wg_of[(m, c)] = wg
@@ -216,14 +218,21 @@ def tile_multiheadselfattention_pa_kernel(tc, x_bytes, x_scale, w_aq, w_ak, out_
                                     start=(k == 0), stop=(k == 2 * G - 1))
 
         def products(b, banks):
-            xy = xy_pool.tile([P, len(banks), 2, CH], F32, name="xy", tag="xy")
-            for k, (i, m, c) in enumerate(banks):
-                acc = project(b, i, m, c)
-                nc.vector.tensor_tensor(out=xy[:, k].rearrange("p q n -> p (q n)"),
-                                        in0=acc[:].rearrange("p (a e) -> p a e", e=HALF).unsqueeze(2).to_broadcast([P, 8, 2, HALF]),
-                                        in1=tab[:, i].unsqueeze(2).to_broadcast([P, 2, 4, D]),
-                                        op=ALU.mult)
+            xy = products_begin(banks)
+            for k, bank in enumerate(banks):
+                one_product(b, bank, xy, k)
             return xy
+
+        def products_begin(banks):
+            return xy_pool.tile([P, len(banks), 2, CH], F32, name="xy", tag="xy")
+
+        def one_product(b, bank, xy, k):
+            i, m, c = bank
+            acc = project(b, i, m, c)
+            nc.vector.tensor_tensor(out=xy[:, k].rearrange("p q n -> p (q n)"),
+                                    in0=acc[:].rearrange("p (a e) -> p a e", e=HALF).unsqueeze(2).to_broadcast([P, 8, 2, HALF]),
+                                    in1=tab[:, i].unsqueeze(2).to_broadcast([P, 2, 4, D]),
+                                    op=ALU.mult)
 
         def store(b, banks, o):
             k = 0
@@ -303,9 +312,12 @@ def tile_multiheadselfattention_pa_kernel(tc, x_bytes, x_scale, w_aq, w_ak, out_
             make_identity(nc, ident[:])
             nc.vector.memset(warm[:], 0.0)
             nc.scalar.activation(out=warm[:], in_=warm[:], func=ACT.Sin)
-            for k in range(6):
+            for k in range(3):
                 w = 2 ** k
                 nc.vector.tensor_scalar(out=ang[:, :, w:2 * w], in0=ang[:, :, 0:w], scalar1=RATIO ** w,
+                                        scalar2=None, op0=ALU.mult)
+            for k in range(1, 8):
+                nc.vector.tensor_scalar(out=ang[:, :, 8 * k:8 * (k + 1)], in0=ang[:, :, 0:8], scalar1=RATIO ** (8 * k),
                                         scalar2=None, op0=ALU.mult)
             nc.vector.tensor_scalar(out=turns[:], in0=ang[:], scalar1=1.0 / TWO_PI, scalar2=0.25,
                                     op0=ALU.mult, op1=ALU.add)
@@ -321,11 +333,8 @@ def tile_multiheadselfattention_pa_kernel(tc, x_bytes, x_scale, w_aq, w_ak, out_
             nc.scalar.activation(out=chh[:], in_=hc[:], func=ACT.Sin)
             x_cast(1)
             x_transpose(1)
-            w_inter(0, 0)
-            x_cast(2)
-            x_transpose(2)
             x_evac_inter(0)
-            x_evac_inter(1)
+            w_inter(0, 0)
             nc.vector.scalar_tensor_tensor(out=sq[:], in0=sh[:], scalar=-2.0, in1=sh[:], op0=ALU.mult, op1=ALU.mult)
             nc.vector.tensor_scalar(out=tab[:].rearrange("p i q (a j) -> p i (q a) j", j=HALF)[:, :, 1:3, :],
                                     in0=sq[:].unsqueeze(2).to_broadcast([P, NT, 2, HALF]), scalar1=1.0, scalar2=None,
@@ -334,17 +343,21 @@ def tile_multiheadselfattention_pa_kernel(tc, x_bytes, x_scale, w_aq, w_ak, out_
                                            op0=ALU.mult, op1=ALU.mult)
             nc.vector.scalar_tensor_tensor(out=tab[:, :, 0, 0:HALF], in0=sh[:], scalar=-2.0, in1=chh[:],
                                            op0=ALU.mult, op1=ALU.mult)
+            x_evac_inter(1)
+            w_quant(0, 0)
+            x_quant(0)
+            x_cast(2)
+            x_transpose(2)
+            x_quant(1)
             for q, op in ((0, ALU.subtract), (1, ALU.add)):
                 nc.vector.scalar_tensor_tensor(out=tab3[:, :, q], in0=tab[:, :, 1, 0:HALF], scalar=-1.0,
                                                in1=tab[:, :, 1, HALF:D], op0=ALU.mult, op1=op)
-            w_quant(0, 0)
-            x_quant(0, n_sets=2)
-            x_evac_inter(2)
             x_cast(3)
-            w_inter(0, 1)
-            xy0 = products(0, [(0, 0, 0)])
+            xy = products(0, [(0, 0, 0)])
             x_transpose(3)
-            add_store(0, [(0, 0, 0)], xy0)
+            add_store(0, [(0, 0, 0)], xy)
+            w_inter(0, 1)
+            x_evac_inter(2)
             x_evac_inter(3)
             x_quant(2, n_sets=2)
             span(0, [(1, 0, 0)])
@@ -398,11 +411,19 @@ def tile_multiheadselfattention_pa_kernel(tc, x_bytes, x_scale, w_aq, w_ak, out_
                     sum_on_tensor(*waiting)
                     for bank, xy in zip(late + [(i + 1, 1, 0)], made):
                         add_store(b, [bank], xy, add_on_vector=True)
+                elif s == NT:
+                    span(b, early)
+                    if s > NT:
+                        sum_on_tensor(*waiting)
+                    waiting = (b, [(i + 1, 1, 0)], products(b, [(i + 1, 1, 0)]))
+                    span(b, late)
+                    x_quant(s + 1)
+                    span3(b, [(i, 1, 1), (i + 1, 1, 1)])
                 else:
                     span(b, early)
                     if s > NT:
                         sum_on_tensor(*waiting)
                     x_quant(s + 1)
-                    span3(b, [(i, 1, 1), (i + 1, 1, 1)])
                     waiting = (b, [(i + 1, 1, 0)], products(b, [(i + 1, 1, 0)]))
+                    span(b, [(i, 1, 1), (i + 1, 1, 1)])
                     span(b, late)

@@ -29,8 +29,8 @@ TWO_PI = 2.0 * PI
 
 SETS = [(0, i, 1) for i in range(NT)] + [(b, i0, 2) for b in range(1, B) for i0 in (0, 2)]
 X_INTER_ON_VECTOR = ()
-W_INTER_ON_GPSIMD = ((0, 0, 0, 0),)
-W_INTER_ON_VECTOR = ((0, 0, 0, 1),)
+W_INTER_ON_GPSIMD = ()
+W_INTER_ON_VECTOR = ((0, 0, 0, 0), (0, 0, 0, 1))
 
 
 def tile_multiheadselfattention_pa_kernel(tc, x_bytes, x_scale, w_aq, w_ak, out_0, out_1):
@@ -333,8 +333,8 @@ def tile_multiheadselfattention_pa_kernel(tc, x_bytes, x_scale, w_aq, w_ak, out_
             nc.scalar.activation(out=chh[:], in_=hc[:], func=ACT.Sin)
             x_cast(1)
             x_transpose(1)
-            x_evac_inter(0)
             w_inter(0, 0)
+            x_evac_inter(0)
             nc.vector.scalar_tensor_tensor(out=sq[:], in0=sh[:], scalar=-2.0, in1=sh[:], op0=ALU.mult, op1=ALU.mult)
             nc.vector.tensor_scalar(out=tab[:].rearrange("p i q (a j) -> p i (q a) j", j=HALF)[:, :, 1:3, :],
                                     in0=sq[:].unsqueeze(2).to_broadcast([P, NT, 2, HALF]), scalar1=1.0, scalar2=None,
@@ -424,6 +424,6 @@ def tile_multiheadselfattention_pa_kernel(tc, x_bytes, x_scale, w_aq, w_ak, out_
                     if s > NT:
                         sum_on_tensor(*waiting)
                     x_quant(s + 1)
+                    span3(b, [(i, 1, 1), (i + 1, 1, 1)])
                     waiting = (b, [(i + 1, 1, 0)], products(b, [(i + 1, 1, 0)]))
-                    span(b, [(i, 1, 1), (i + 1, 1, 1)])
                     span(b, late)

@@ -333,6 +333,9 @@ def tile_multiheadselfattention_pa_kernel(tc, x_bytes, x_scale, w_aq, w_ak, out_
             nc.scalar.activation(out=chh[:], in_=hc[:], func=ACT.Sin)
             x_cast(1)
             x_transpose(1)
+            busy = psu.tile([P, CH], F32, name="acc", tag="acc")
+            for k in range(4):
+                nc.tensor.matmul(busy[:], lhsT=xw_of[0][:, 0:P], rhs=xw_of[0][:, 0:CH], start=True, stop=True)
             w_inter(0, 0)
             x_evac_inter(0)
             nc.vector.scalar_tensor_tensor(out=sq[:], in0=sh[:], scalar=-2.0, in1=sh[:], op0=ALU.mult, op1=ALU.mult)
@@ -343,15 +346,12 @@ def tile_multiheadselfattention_pa_kernel(tc, x_bytes, x_scale, w_aq, w_ak, out_
                                            op0=ALU.mult, op1=ALU.mult)
             nc.vector.scalar_tensor_tensor(out=tab[:, :, 0, 0:HALF], in0=sh[:], scalar=-2.0, in1=chh[:],
                                            op0=ALU.mult, op1=ALU.mult)
+            x_quant(0)
             x_evac_inter(1)
             w_quant(0, 0)
-            x_quant(0)
             x_cast(2)
             x_transpose(2)
             x_quant(1)
-            for q, op in ((0, ALU.subtract), (1, ALU.add)):
-                nc.vector.scalar_tensor_tensor(out=tab3[:, :, q], in0=tab[:, :, 1, 0:HALF], scalar=-1.0,
-                                               in1=tab[:, :, 1, HALF:D], op0=ALU.mult, op1=op)
             x_cast(3)
             xy = products(0, [(0, 0, 0)])
             x_transpose(3)
@@ -379,11 +379,15 @@ def tile_multiheadselfattention_pa_kernel(tc, x_bytes, x_scale, w_aq, w_ak, out_
             span(0, [(2, 1, 0), (3, 1, 0)])
             x_cast(4)
             x_transpose(4)
+            x_evac(4)
             load_x(2, 2, 0, NT * M)
-            x_evac_inter(4)
-            span3(0, [(0, 1, 1), (1, 1, 1)])
+            x_inter(4)
+            span(0, [(0, 1, 1), (1, 1, 1)])
             x_quant(4)
-            span3(0, [(2, 1, 1), (3, 1, 1)])
+            span(0, [(2, 1, 1), (3, 1, 1)])
+            for q, op in ((0, ALU.subtract), (1, ALU.add)):
+                nc.vector.scalar_tensor_tensor(out=tab3[:, :, q], in0=tab[:, :, 1, 0:HALF], scalar=-1.0,
+                                               in1=tab[:, :, 1, HALF:D], op0=ALU.mult, op1=op)
             x_cast(5)
             x_transpose(5)
             x_evac(5)
@@ -407,9 +411,11 @@ def tile_multiheadselfattention_pa_kernel(tc, x_bytes, x_scale, w_aq, w_ak, out_
                     sum_on_tensor(*waiting)
                     waiting = (b, early[2:], products(b, early[2:]))
                     span(b, early[:2])
-                    made = [products(b, [bank]) for bank in late + [(i + 1, 1, 0)]]
+                    span(b, late[:1])
+                    rest = [late[1], (i + 1, 1, 0)]
+                    made = [products(b, [bank]) for bank in rest]
                     sum_on_tensor(*waiting)
-                    for bank, xy in zip(late + [(i + 1, 1, 0)], made):
+                    for bank, xy in zip(rest, made):
                         add_store(b, [bank], xy, add_on_vector=True)
                 elif s == NT:
                     span(b, early)

@@ -28,7 +28,6 @@ PI = 3.141592653589793
 TWO_PI = 2.0 * PI
 
 SETS = [(0, i, 1) for i in range(NT)] + [(b, i0, 2) for b in range(1, B) for i0 in (0, 2)]
-X_INTER_ON_VECTOR = ()
 W_INTER_ON_GPSIMD = ()
 W_INTER_ON_VECTOR = ((0, 0, 0, 0), (0, 0, 0, 1))
 
@@ -112,12 +111,12 @@ def tile_multiheadselfattention_pa_kernel(tc, x_bytes, x_scale, w_aq, w_ak, out_
                                         words[:, lo:ii * (M // 2) + 256 * (g + 1):2], ident[:])
             xbank_of[s] = banks
 
-        def x_evac(s):
+        def x_evac(s, passes=(0, 1)):
             b, i0, n = SETS[s]
             R = n * P
             per = 2
             xp = xp_pool.tile([P, G, 4, R], BF16, name="xp", tag="xp")
-            for q in range(4):
+            for q in range(2 * passes[0], 2 * passes[-1] + 2):
                 g, u = q // 2, q % 2
                 off = (q % per) * R
                 pairs = xbank_of[s][q // per][:, off:off + R].bitcast(BF16).rearrange("p (r e) -> p r e", e=2)
@@ -127,34 +126,31 @@ def tile_multiheadselfattention_pa_kernel(tc, x_bytes, x_scale, w_aq, w_ak, out_
                                          scale=xs[:, g, t:t + 1])
             xp_of[s] = xp
 
-        def x_evac_inter(s):
+        def x_evac_inter(s, passes=(0, 1)):
             b, i0, n = SETS[s]
             R = n * P
             if s == 2:
                 xg_of[2] = xg_of[3] = xg_pool.tile([P, G, 2 * P, 4], BF16, name="xg", tag="xg", align_bytes=64)
-            elif s != 3:
+            elif s != 3 and s not in xg_of:
                 xg_of[s] = xg_pool.tile([P, G, R, 4], BF16, name="xg", tag="xg", align_bytes=64)
             xg, lo = xg_of[s], P if s == 3 else 0
-            for g in range(G):
+            for g in passes:
                 words = xbank_of[s][g][:, :2 * R]
                 nc.vector.tensor_tensor(out=xg[:, g, lo:lo + R].rearrange("p r (u e) -> p r u e", e=2),
                                         in0=words.bitcast(BF16).rearrange("p (u r e) -> p r u e", u=2, e=2),
                                         in1=xs[:, g, :].rearrange("p (u e) -> p u e", e=2).unsqueeze(1).to_broadcast([P, R, 2, 2]),
                                         op=ALU.mult)
 
-        def x_inter(s):
+        def x_inter(s, passes=(0, 1)):
             b, i0, n = SETS[s]
             R = n * P
             xp = xp_of[s]
-            xg = xg_pool.tile([P, G, R, 4], BF16, name="xg", tag="xg", align_bytes=64)
-            for g in range(G):
-                src = xp[:, g].rearrange("p t (c i) -> p c t i", i=4)
-                dst = xg[:, g].rearrange("p (c i) t -> p c t i", i=4)
-                if s in X_INTER_ON_VECTOR:
-                    nc.vector.tensor_copy(out=dst, in_=src)
-                else:
-                    nc.scalar.copy(out=dst, in_=src)
-            xg_of[s] = xg
+            if s not in xg_of:
+                xg_of[s] = xg_pool.tile([P, G, R, 4], BF16, name="xg", tag="xg", align_bytes=64)
+            xg = xg_of[s]
+            for g in passes:
+                nc.scalar.copy(out=xg[:, g].rearrange("p (c i) t -> p c t i", i=4),
+                               in_=xp[:, g].rearrange("p t (c i) -> p c t i", i=4))
 
         def x_quant(s, n_sets=1):
             b, i0, n = SETS[s]
@@ -352,6 +348,9 @@ def tile_multiheadselfattention_pa_kernel(tc, x_bytes, x_scale, w_aq, w_ak, out_
             x_cast(2)
             x_transpose(2)
             x_quant(1)
+            for q, op in ((0, ALU.subtract), (1, ALU.add)):
+                nc.vector.scalar_tensor_tensor(out=tab3[:, :, q], in0=tab[:, :, 1, 0:HALF], scalar=-1.0,
+                                               in1=tab[:, :, 1, HALF:D], op0=ALU.mult, op1=op)
             x_cast(3)
             xy = products(0, [(0, 0, 0)])
             x_transpose(3)
@@ -379,15 +378,13 @@ def tile_multiheadselfattention_pa_kernel(tc, x_bytes, x_scale, w_aq, w_ak, out_
             span(0, [(2, 1, 0), (3, 1, 0)])
             x_cast(4)
             x_transpose(4)
-            x_evac(4)
+            x_evac(4, (1,))
             load_x(2, 2, 0, NT * M)
-            x_inter(4)
+            x_evac_inter(4, (0,))
+            x_inter(4, (1,))
             span(0, [(0, 1, 1), (1, 1, 1)])
             x_quant(4)
             span(0, [(2, 1, 1), (3, 1, 1)])
-            for q, op in ((0, ALU.subtract), (1, ALU.add)):
-                nc.vector.scalar_tensor_tensor(out=tab3[:, :, q], in0=tab[:, :, 1, 0:HALF], scalar=-1.0,
-                                               in1=tab[:, :, 1, HALF:D], op0=ALU.mult, op1=op)
             x_cast(5)
             x_transpose(5)
             x_evac(5)
@@ -408,13 +405,12 @@ def tile_multiheadselfattention_pa_kernel(tc, x_bytes, x_scale, w_aq, w_ak, out_
                 late = [(i + 1, 0, 0), (i + 1, 0, 1)]
                 if s == last:
                     span3(b, [(i, 1, 1), (i + 1, 1, 1)])
-                    sum_on_tensor(*waiting)
-                    waiting = (b, early[2:], products(b, early[2:]))
+                    later = (b, early[2:], products(b, early[2:]))
                     span(b, early[:2])
-                    span(b, late[:1])
-                    rest = [late[1], (i + 1, 1, 0)]
-                    made = [products(b, [bank]) for bank in rest]
                     sum_on_tensor(*waiting)
+                    rest = late + [(i + 1, 1, 0)]
+                    made = [products(b, [bank]) for bank in rest]
+                    sum_on_tensor(*later)
                     for bank, xy in zip(rest, made):
                         add_store(b, [bank], xy, add_on_vector=True)
                 elif s == NT:

from contextlib import ExitStack

import concourse.mybir as mybir
from concourse.masks import make_identity

B, T, M, H, D = 4, 512, 1024, 8, 128
HD = H * D
FLOPS = 2 * (B * T) * M * (2 * HD)

F32 = mybir.dt.float32
BF16 = mybir.dt.bfloat16
I32 = mybir.dt.int32
U32 = mybir.dt.uint32
U8 = mybir.dt.uint8
FP8 = mybir.dt.float8_e4m3fn
FP8X4 = mybir.dt.float8_e4m3fn_x4
ALU = mybir.AluOpType
ACT = mybir.ActivationFunctionType
ENG = mybir.EngineType

P = 128
NT = 4
G = 2
CH = 512
HALF = D // 2
RATIO = 10000.0 ** (-1.0 / HALF)
PI = 3.141592653589793
TWO_PI = 2.0 * PI

SETS = [(0, i, 1) for i in range(NT)] + [(b, i0, 2) for b in range(1, B) for i0 in (0, 2)]
W_INTER_ON_GPSIMD = ()
W_INTER_ON_VECTOR = ((0, 0, 0, 0), (0, 0, 0, 1))


def tile_multiheadselfattention_pa_kernel(tc, x_bytes, x_scale, w_aq, w_ak, out_0, out_1):
    nc = tc.nc
    with ExitStack() as ctx:
        const = ctx.enter_context(tc.tile_pool(name="const", bufs=1))
        xb_pool = ctx.enter_context(tc.tile_pool(name="xb", bufs=3))
        wr_pool = ctx.enter_context(tc.tile_pool(name="wr", bufs=4))
        xw_pool = ctx.enter_context(tc.tile_pool(name="xw", bufs=3))
        xp_pool = ctx.enter_context(tc.tile_pool(name="xp", bufs=3))
        xg_pool = ctx.enter_context(tc.tile_pool(name="xg", bufs=3))
        wg_pool = ctx.enter_context(tc.tile_pool(name="wg", bufs=2))
        xy_pool = ctx.enter_context(tc.tile_pool(name="xy", bufs=4))
        x3_pool = ctx.enter_context(tc.tile_pool(name="x3", bufs=2))
        o_pool = ctx.enter_context(tc.tile_pool(name="o", bufs=6))
        psx = ctx.enter_context(tc.psum_pool(name="psx", bufs=3))
        psu = ctx.enter_context(tc.psum_pool(name="psu", bufs=5))

        xv = x_bytes.rearrange("b (p i) k -> b p (i k)", i=NT)
        wv = [w.rearrange("(g p j) h d -> g p j (h d)", g=G, p=P, j=4) for w in (w_aq, w_ak)]
        ov = [o.rearrange("b (p i) h d -> b i p (h d)", i=NT) for o in (out_0, out_1)]

        xb_of = {}
        wr = {}

        def load_x(key, b, lo, hi):
            xb_of[key] = xb_pool.tile([P, hi - lo], U8, name="xbytes", tag="xbytes")
            nc.sync.dma_start(out=xb_of[key][:], in_=xv[b][:, lo:hi])

        def load_w(m, c, passes=(0, 1)):
            for g in passes:
                wr[(m, g, c)] = wr_pool.tile([P, 4, CH], BF16, name="wr", tag="wr")
                nc.sync.dma_start(out=wr[(m, g, c)][:], in_=wv[m][g][:, :, c * CH:(c + 1) * CH])

        def bytes_of(b, i0, n):
            if b > 0:
                return xb_of[b][:, i0 * M:(i0 + n) * M]
            if i0 == 0:
                return xb_of["a"][:]
            return xb_of["b"][:, (i0 - 1) * M:(i0 - 1 + n) * M]

        xs = const.tile([P, G, 4], F32, name="xs")
        load_x("a", 0, 0, M)
        nc.sync.dma_start(out=xs[:], in_=x_scale[0, 0, :].rearrange("(g p t) -> p g t", g=G, p=P, t=4))
        load_w(0, 0, (0,))
        load_x("b", 0, M, NT * M)
        load_w(0, 0, (1,))
        load_w(0, 1)

        xw_of = {}
        xbank_of = {}
        xp_of = {}
        xg_of = {}
        xc_of = {}

        def x_cast(s):
            b, i0, n = SETS[s]
            xw_of[s] = xw_pool.tile([P, n * M], BF16, name="xw", tag="xw")
            parts = 2 if s == 0 else 1
            w = n * M // parts
            for k in range(parts):
                nc.scalar.copy(out=xw_of[s][:, k * w:(k + 1) * w], in_=bytes_of(b, i0, n)[:, k * w:(k + 1) * w].bitcast(FP8))

        def x_transpose(s):
            b, i0, n = SETS[s]
            R = n * P
            words = xw_of[s][:].bitcast(F32)
            per = 2
            banks = []
            for q in range(4):
                g, u = q // 2, q % 2
                if q % per == 0:
                    bank = psx.tile([P, CH], F32, name="xbank", tag="xbank")
                    banks.append(bank)
                off = (q % per) * R
                for ii in range(n):
                    lo = ii * (M // 2) + 256 * g + u
                    nc.tensor.transpose(banks[-1][:, off + ii * P:off + (ii + 1) * P],
                                        words[:, lo:ii * (M // 2) + 256 * (g + 1):2], ident[:])
            xbank_of[s] = banks

        def x_evac(s, passes=(0, 1)):
            b, i0, n = SETS[s]
            R = n * P
            per = 2
            xp = xp_pool.tile([P, G, 4, R], BF16, name="xp", tag="xp")
            for q in range(2 * passes[0], 2 * passes[-1] + 2):
                g, u = q // 2, q % 2
                off = (q % per) * R
                pairs = xbank_of[s][q // per][:, off:off + R].bitcast(BF16).rearrange("p (r e) -> p r e", e=2)
                for e in range(2):
                    t = 2 * u + e
                    nc.scalar.activation(out=xp[:, g, t, :], in_=pairs[:, :, e], func=ACT.Copy,
                                         scale=xs[:, g, t:t + 1])
            xp_of[s] = xp

        def x_evac_inter(s, passes=(0, 1)):
            b, i0, n = SETS[s]
            R = n * P
            if s == 2:
                xg_of[2] = xg_of[3] = xg_pool.tile([P, G, 2 * P, 4], BF16, name="xg", tag="xg", align_bytes=64)
            elif s != 3 and s not in xg_of:
                xg_of[s] = xg_pool.tile([P, G, R, 4], BF16, name="xg", tag="xg", align_bytes=64)
            xg, lo = xg_of[s], P if s == 3 else 0
            for g in passes:
                words = xbank_of[s][g][:, :2 * R]
                nc.vector.tensor_tensor(out=xg[:, g, lo:lo + R].rearrange("p r (u e) -> p r u e", e=2),
                                        in0=words.bitcast(BF16).rearrange("p (u r e) -> p r u e", u=2, e=2),
                                        in1=xs[:, g, :].rearrange("p (u e) -> p u e", e=2).unsqueeze(1).to_broadcast([P, R, 2, 2]),
                                        op=ALU.mult)

        def x_inter(s, passes=(0, 1)):
            b, i0, n = SETS[s]
            R = n * P
            xp = xp_of[s]
            if s not in xg_of:
                xg_of[s] = xg_pool.tile([P, G, R, 4], BF16, name="xg", tag="xg", align_bytes=64)
            xg = xg_of[s]
            for g in passes:
                nc.scalar.copy(out=xg[:, g].rearrange("p (c i) t -> p c t i", i=4),
                               in_=xp[:, g].rearrange("p t (c i) -> p c t i", i=4))

        def x_quant(s, n_sets=1):
            b, i0, n = SETS[s]
            n = n * n_sets
            R = n * P
            xc = const.tile([P, G, R], U32, name="xc%d" % s, align_bytes=64)
            xsc = const.tile([P, G, R], U8, name="xsc%d" % s, align_bytes=64)
            nc.vector.quantize_mx(out=xc[:].rearrange("p g r -> p (g r)").bitcast(FP8X4),
                                  scales=xsc[:].rearrange("p g r -> p (g r)"),
                                  in_=xg_of[s][:].rearrange("p g r t -> p (g r t)"))
            for ii in range(n):
                xc_of[(b, i0 + ii)] = (xc, xsc, ii * P)

        wg_of = {}
        wc_of = {}

        def w_inter(m, c):
            wg = wg_pool.tile([P, G, CH, 4], BF16, name="wg", tag="wg", align_bytes=64)
            for g in range(G):
                for f in range(2):
                    src = wr[(m, g, c)][:].rearrange("p j (h f a i) -> p f h a j i", f=2, a=HALF // 4, i=4)[:, 1 - f]
                    dst = wg[:, g].rearrange("p (f h a i) j -> p f h a j i", f=2, a=HALF // 4, i=4)[:, f]
                    if (m, c, g, f) in W_INTER_ON_GPSIMD:
                        nc.gpsimd.tensor_scalar(out=wg[:, g, f * 256:(f + 1) * 256].rearrange("p (h e) j -> p h e j", e=HALF),
                                                in0=wr[(m, g, c)][:].rearrange("p j (h f e) -> p f h e j", f=2, e=HALF)[:, 1 - f],
                                                scalar1=1.0, scalar2=0.0, op0=ALU.mult, op1=ALU.add)
                    elif (m, c, g, f) in W_INTER_ON_VECTOR:
                        nc.vector.tensor_copy(out=dst, in_=src)
                    else:
                        nc.scalar.copy(out=dst, in_=src)
            wg_of[(m, c)] = wg

        def w_quant(m, c):
            wc = const.tile([P, G, CH], U32, name="wc%d%d" % (m, c), align_bytes=64)
            wsc = const.tile([P, G, CH], U8, name="wsc%d%d" % (m, c), align_bytes=64)
            nc.vector.quantize_mx(out=wc[:].rearrange("p g n -> p (g n)").bitcast(FP8X4),
                                  scales=wsc[:].rearrange("p g n -> p (g n)"),
                                  in_=wg_of[(m, c)][:].rearrange("p g n j -> p (g n j)"))
            wc_of[(m, c)] = (wc, wsc)

        def project(b, i, m, c):
            xc, xsc, off = xc_of[(b, i)]
            wc, wsc = wc_of[(m, c)]
            acc = psu.tile([P, CH], F32, name="acc", tag="acc")
            for g in range(G):
                nc.tensor.matmul_mx(out=acc[:],
                                    lhsT=xc[:, g, off:off + P].bitcast(FP8X4), lhsT_scale=xsc[:, g, off:off + P],
                                    rhs=wc[:, g, :].bitcast(FP8X4), rhs_scale=wsc[:, g, :],
                                    start=(g == 0), stop=(g == G - 1))
            return acc

        def half_sums(b, i, m, c, out):
            xc, xsc, off = xc_of[(b, i)]
            wc, wsc = wc_of[(m, c)]
            for k in range(2 * G):
                g, f = k // 2, k % 2
                nc.tensor.matmul_mx(out=out,
                                    lhsT=xc[:, g, off:off + P].bitcast(FP8X4), lhsT_scale=xsc[:, g, off:off + P],
                                    rhs=wc[:, g, f * 256:(f + 1) * 256].bitcast(FP8X4),
                                    rhs_scale=wsc[:, g, f * 256:(f + 1) * 256],
                                    start=(k == 0), stop=(k == 2 * G - 1))

        def products(b, banks):
            xy = products_begin(banks)
            for k, bank in enumerate(banks):
                one_product(b, bank, xy, k)
            return xy

        def products_begin(banks):
            return xy_pool.tile([P, len(banks), 2, CH], F32, name="xy", tag="xy")

        def one_product(b, bank, xy, k):
            i, m, c = bank
            acc = project(b, i, m, c)
            nc.vector.tensor_tensor(out=xy[:, k].rearrange("p q n -> p (q n)"),
                                    in0=acc[:].rearrange("p (a e) -> p a e", e=HALF).unsqueeze(2).to_broadcast([P, 8, 2, HALF]),
                                    in1=tab[:, i].unsqueeze(2).to_broadcast([P, 2, 4, D]),
                                    op=ALU.mult)

        def store(b, banks, o):
            k = 0
            while k < len(banks):
                i, m, c = banks[k]
                n = 1
                while k + n < len(banks) and banks[k + n] == (i, m, c + n):
                    n += 1
                nc.sync.dma_start(out=ov[m][b, i][:, c * CH:(c + n) * CH], in_=o[:, k * CH:(k + n) * CH])
                k += n

        def add_store(b, banks, xy, add_on_vector=False):
            o = o_pool.tile([P, len(banks) * CH], F32, name="o", tag="o")
            eng = nc.vector if add_on_vector else nc.gpsimd
            eng.tensor_tensor(out=o[:].rearrange("p (k n) -> p k n", n=CH),
                              in0=xy[:, :, 0, :], in1=xy[:, :, 1, :], op=ALU.add)
            store(b, banks, o)

        def span(b, banks):
            add_store(b, banks, products(b, banks))

        def products3(b, banks):
            sums = psu.tile([P, CH], F32, name="acc", tag="acc")
            k3 = x3_pool.tile([P, 2, 4, HALF], F32, name="k3", tag="k3")
            kk = x3_pool.tile([P, 2, 4, 2, HALF], F32, name="kk", tag="kk")
            for k, (i, m, c) in enumerate(banks):
                acc = project(b, i, m, c)
                half_sums(b, i, m, c, sums[:, k * 256:(k + 1) * 256])
                nc.vector.tensor_tensor(out=kk[:, k].rearrange("p h q e -> p q h e"),
                                        in0=acc[:].rearrange("p (q h e) -> p q h e", q=2, e=HALF),
                                        in1=tab3[:, i].unsqueeze(2).to_broadcast([P, 2, 4, HALF]),
                                        op=ALU.mult)
            i0, i1 = banks[0][0], banks[1][0]
            cos = tab[:, i0:i1 + 1, 0, HALF:D]
            if i0 == i1:
                cos = cos.to_broadcast([P, 2, HALF])
            nc.vector.tensor_tensor(out=k3[:], in0=sums[:].rearrange("p (k h e) -> p k h e", k=2, e=HALF),
                                    in1=cos.unsqueeze(2).to_broadcast([P, 2, 4, HALF]), op=ALU.mult)
            return k3, kk

        def add_store3(b, banks, k3, kk, add_on_vector=False):
            o = o_pool.tile([P, 2 * CH], F32, name="o", tag="o")
            eng = nc.vector if add_on_vector else nc.gpsimd
            eng.tensor_tensor(out=o[:].rearrange("p (a q e) -> p a q e", q=2, e=HALF),
                                    in0=k3[:].rearrange("p k h e -> p (k h) e").unsqueeze(2).to_broadcast([P, 8, 2, HALF]),
                                    in1=kk[:].rearrange("p k h q e -> p (k h) q e"), op=ALU.add)
            store(b, banks, o)

        def span3(b, banks):
            add_store3(b, banks, *products3(b, banks))

        def sum_on_tensor(b, banks, xy):
            o = o_pool.tile([P, len(banks) * CH], F32, name="o", tag="o")
            for k in range(len(banks)):
                bank = psx.tile([P, CH], F32, name="xbank", tag="xbank")
                for q in range(2):
                    nc.tensor.matmul(bank[:], lhsT=ident[:], rhs=xy[:, k, q, :], start=(q == 0), stop=(q == 1))
                nc.scalar.copy(out=o[:, k * CH:(k + 1) * CH], in_=bank[:])
            store(b, banks, o)

        ident = const.tile([P, P], F32, name="ident")
        warm = const.tile([P, 1], F32, name="warm")
        ang = const.tile([P, NT, HALF], F32, name="ang")
        turns = const.tile([P, NT, HALF], I32, name="turns")
        red = const.tile([P, NT, HALF], F32, name="red")
        sh = const.tile([P, NT, HALF], F32, name="sh")
        mag = const.tile([P, NT, HALF], F32, name="mag")
        hc = const.tile([P, NT, HALF], F32, name="hc")
        chh = const.tile([P, NT, HALF], F32, name="chh")
        sq = const.tile([P, NT, HALF], F32, name="sq")
        tab = const.tile([P, NT, 2, D], F32, name="tab")
        tab3 = const.tile([P, NT, 2, HALF], F32, name="tab3")

        with tc.manual_schedule(engines={ENG.PE, ENG.DVE, ENG.Activation, ENG.Pool}):
            nc.gpsimd.iota(ang[:, :, 0:1], pattern=[[1, NT]], base=0, channel_multiplier=NT,
                           allow_small_or_imprecise_dtypes=True)
            make_identity(nc, ident[:])
            nc.vector.memset(warm[:], 0.0)
            nc.scalar.activation(out=warm[:], in_=warm[:], func=ACT.Sin)
            for k in range(3):
                w = 2 ** k
                nc.vector.tensor_scalar(out=ang[:, :, w:2 * w], in0=ang[:, :, 0:w], scalar1=RATIO ** w,
                                        scalar2=None, op0=ALU.mult)
            for k in range(1, 8):
                nc.vector.tensor_scalar(out=ang[:, :, 8 * k:8 * (k + 1)], in0=ang[:, :, 0:8], scalar1=RATIO ** (8 * k),
                                        scalar2=None, op0=ALU.mult)
            nc.vector.tensor_scalar(out=turns[:], in0=ang[:], scalar1=1.0 / TWO_PI, scalar2=0.25,
                                    op0=ALU.mult, op1=ALU.add)
            nc.vector.scalar_tensor_tensor(out=red[:], in0=turns[:], scalar=-TWO_PI, in1=ang[:],
                                           op0=ALU.mult, op1=ALU.add)
            nc.vector.scalar_tensor_tensor(out=mag[:], in0=red[:], scalar=-1.0, in1=red[:],
                                           op0=ALU.mult, op1=ALU.max)
            nc.vector.tensor_scalar(out=hc[:], in0=mag[:], scalar1=-0.5, scalar2=0.5 * PI,
                                    op0=ALU.mult, op1=ALU.add)
            x_cast(0)
            x_transpose(0)
            nc.scalar.activation(out=sh[:], in_=red[:], func=ACT.Sin, scale=0.5)
            nc.scalar.activation(out=chh[:], in_=hc[:], func=ACT.Sin)
            x_cast(1)
            x_transpose(1)
            busy = psu.tile([P, CH], F32, name="acc", tag="acc")
            for k in range(4):
                nc.tensor.matmul(busy[:], lhsT=xw_of[0][:, 0:P], rhs=xw_of[0][:, 0:CH], start=True, stop=True)
            w_inter(0, 0)
            x_evac_inter(0)
            nc.vector.scalar_tensor_tensor(out=sq[:], in0=sh[:], scalar=-2.0, in1=sh[:], op0=ALU.mult, op1=ALU.mult)
            nc.vector.tensor_scalar(out=tab[:].rearrange("p i q (a j) -> p i (q a) j", j=HALF)[:, :, 1:3, :],
                                    in0=sq[:].unsqueeze(2).to_broadcast([P, NT, 2, HALF]), scalar1=1.0, scalar2=None,
                                    op0=ALU.add)
            nc.vector.scalar_tensor_tensor(out=tab[:, :, 1, HALF:D], in0=sh[:], scalar=2.0, in1=chh[:],
                                           op0=ALU.mult, op1=ALU.mult)
            nc.vector.scalar_tensor_tensor(out=tab[:, :, 0, 0:HALF], in0=sh[:], scalar=-2.0, in1=chh[:],
                                           op0=ALU.mult, op1=ALU.mult)
            x_quant(0)
            x_evac_inter(1)
            w_quant(0, 0)
            x_cast(2)
            x_transpose(2)
            x_quant(1)
            for q, op in ((0, ALU.subtract), (1, ALU.add)):
                nc.vector.scalar_tensor_tensor(out=tab3[:, :, q], in0=tab[:, :, 1, 0:HALF], scalar=-1.0,
                                               in1=tab[:, :, 1, HALF:D], op0=ALU.mult, op1=op)
            x_cast(3)
            xy = products(0, [(0, 0, 0)])
            x_transpose(3)
            add_store(0, [(0, 0, 0)], xy)
            w_inter(0, 1)
            x_evac_inter(2)
            x_evac_inter(3)
            x_quant(2, n_sets=2)
            span(0, [(1, 0, 0)])
            span(0, [(2, 0, 0)])
            w_quant(0, 1)
            span(0, [(3, 0, 0)])

        load_w(1, 0)
        load_x(1, 1, 0, NT * M)
        load_w(1, 1)
        with tc.manual_schedule(engines={ENG.DVE}):
            w_inter(1, 0)
            span(0, [(0, 0, 1), (1, 0, 1)])
            w_quant(1, 0)
            span(0, [(2, 0, 1), (3, 0, 1)])
            w_inter(1, 1)
            span(0, [(0, 1, 0), (1, 1, 0)])
            w_quant(1, 1)
            span(0, [(2, 1, 0), (3, 1, 0)])
            x_cast(4)
            x_transpose(4)
            x_evac(4, (1,))
            load_x(2, 2, 0, NT * M)
            x_evac_inter(4, (0,))
            x_inter(4, (1,))
            span(0, [(0, 1, 1), (1, 1, 1)])
            x_quant(4)
            span(0, [(2, 1, 1), (3, 1, 1)])
            x_cast(5)
            x_transpose(5)
            x_evac(5)

        load_x(3, 3, 0, NT * M)
        last = len(SETS) - 1
        with tc.manual_schedule(engines={ENG.DVE}):
            for s in range(NT, len(SETS)):
                b, i0, n = SETS[s]
                if s + 1 < len(SETS):
                    x_inter(s + 1)
                if s + 2 < len(SETS):
                    x_cast(s + 2)
                    x_transpose(s + 2)
                    x_evac(s + 2)
                i = i0
                early = [(i, 0, 0), (i, 0, 1), (i, 1, 0)]
                late = [(i + 1, 0, 0), (i + 1, 0, 1)]
                if s == last:
                    span3(b, [(i, 1, 1), (i + 1, 1, 1)])
                    later = (b, early[2:], products(b, early[2:]))
                    span(b, early[:2])
                    sum_on_tensor(*waiting)
                    rest = late + [(i + 1, 1, 0)]
                    made = [products(b, [bank]) for bank in rest]
                    sum_on_tensor(*later)
                    for bank, xy in zip(rest, made):
                        add_store(b, [bank], xy, add_on_vector=True)
                elif s == NT:
                    span(b, early)
                    if s > NT:
                        sum_on_tensor(*waiting)
                    waiting = (b, [(i + 1, 1, 0)], products(b, [(i + 1, 1, 0)]))
                    span(b, late)
                    x_quant(s + 1)
                    span3(b, [(i, 1, 1), (i + 1, 1, 1)])
                else:
                    span(b, early)
                    if s > NT:
                        sum_on_tensor(*waiting)
                    x_quant(s + 1)
                    span3(b, [(i, 1, 1), (i + 1, 1, 1)])
                    waiting = (b, [(i + 1, 1, 0)], products(b, [(i + 1, 1, 0)]))
                    span(b, late)
